import numpy as np
import ml_dtypes


def mxq(x, axis, fmt="e4m3"):
    dtype, down = {"e4m3": (ml_dtypes.float8_e4m3fn, 7), "e5m2": (ml_dtypes.float8_e5m2, 14)}[fmt]
    v = np.moveaxis(np.asarray(x, np.float32).astype(ml_dtypes.bfloat16).astype(np.float64), axis, -1)
    blocks = v.reshape(v.shape[:-1] + (-1, 32))
    amax = np.abs(blocks).max(-1, keepdims=True)
    byte = np.maximum(np.where(amax > 0, np.frexp(amax)[1] - 1 + 127, 0) - down, 1)
    scale = np.exp2(byte - 127.0)
    codes = (blocks / scale).astype(np.float32).astype(dtype).astype(np.float64)
    return np.moveaxis((codes * scale).reshape(v.shape), -1, axis)


WIDE = False


def mx_kscale(k):
    if not WIDE:
        return np.ones(k)
    levels = np.array([10, -10, 5, -5, 0])
    a = np.random.permutation(np.resize(levels, k // 512 * 4)).reshape(k // 512, 4)
    idx = np.arange(k)
    return np.exp2(a[idx // 512, idx % 128 // 32])


BF16 = ml_dtypes.bfloat16


def bf(x):
    return np.asarray(x, np.float32).astype(BF16)


def f64(x):
    return np.asarray(x).astype(np.float64)


B, L, D, E, S, H = 4, 2048, 512, 16, 32, 512
K = E * S


def softmax(v):
    e = np.exp(v - v.max(-1, keepdims=True))
    return e / e.sum(-1, keepdims=True)


def setup_inputs():
    s = mx_kscale(H)
    return {"h": bf(np.random.standard_normal((B, E, S, H)) * 0.6 * s),
            "w2": bf(np.random.standard_normal((E, H, D)) * 1.5 / np.sqrt(H) / s[:, None]),
            "b2": bf(np.random.standard_normal((E, D)) * 0.5),
            "logits": bf(np.random.standard_normal((B, L, E, S)) * 2.0)}


def reference(h, w2, b2, logits):
    eo = (mxq(f64(h), 3, "e4m3") @ mxq(f64(w2), 1, "e4m3")) + f64(b2)[:, None, :]
    eo = eo.reshape(B, K, D)
    c_w = softmax(f64(logits).reshape(B, L, K))
    return mxq(c_w, 2, "e4m3") @ mxq(eo, 1, "e4m3")

@@ -1,0 +1,209 @@
+from contextlib import ExitStack
+
+import concourse.mybir as mybir
+from concourse.masks import make_identity
+
+BF16 = mybir.dt.bfloat16
+F32 = mybir.dt.float32
+U32 = mybir.dt.uint32
+U8 = mybir.dt.uint8
+FP8X4 = mybir.dt.float8_e4m3fn_x4
+ALU = mybir.AluOpType
+ACT = mybir.ActivationFunctionType
+AX = mybir.AxisListType
+
+P = 128
+B, L, D, E, S, H = 4, 2048, 512, 16, 32, 512
+K = E * S
+FLOPS = 2 * B * E * S * H * D + 2 * B * L * K * D
+TPC = 4
+NCH = B * L // (P * TPC)
+CPB = NCH // B
+
+
+def tile_softmoe_pb_t_kernel(tc, h, w2, b2, logits, out):
+    nc = tc.nc
+    with ExitStack() as ctx:
+        const = ctx.enter_context(tc.tile_pool(name="const", bufs=1))
+        hpool = ctx.enter_context(tc.tile_pool(name="hpool", bufs=2))
+        wpool = ctx.enter_context(tc.tile_pool(name="wpool", bufs=3))
+        wgpool = ctx.enter_context(tc.tile_pool(name="wgpool", bufs=2))
+        xpool = ctx.enter_context(tc.tile_pool(name="xpool", bufs=4))
+        tree = ctx.enter_context(tc.tile_pool(name="tree", bufs=2))
+        stat = ctx.enter_context(tc.tile_pool(name="stat", bufs=3))
+        work = ctx.enter_context(tc.tile_pool(name="work", bufs=2))
+        opool = ctx.enter_context(tc.tile_pool(name="opool", bufs=3))
+        pstr = ctx.enter_context(tc.psum_pool(name="pstr", bufs=4))
+        psmm = ctx.enter_context(tc.psum_pool(name="psmm", bufs=4))
+
+        ident_bf = const.tile([P, P], BF16)
+        make_identity(nc, ident_bf[:])
+        ident_f = const.tile([P, P], F32)
+        make_identity(nc, ident_f[:])
+
+        hq = const.tile([P, E * P], U32, align_bytes=64)
+        hs = const.tile([P, E * P], U8, align_bytes=64)
+        eoT = const.tile([P, 4, B, K], BF16)
+        eoq = const.tile([P, B * D], U32, align_bytes=64)
+        eos = const.tile([P, B * D], U8, align_bytes=64)
+        cwq = const.tile([P, NCH * TPC * P], U32, align_bytes=64)
+        cws = const.tile([P, NCH * TPC * P], U8, align_bytes=64)
+
+        def copy_on(scalar_engine, dst, src):
+            if scalar_engine:
+                nc.scalar.copy(out=dst, in_=src)
+            else:
+                nc.vector.tensor_copy(out=dst, in_=src)
+
+        b2pad = const.tile([P, D], BF16)
+        nc.gpsimd.memset(b2pad[:], 0.0)
+        nc.sync.dma_start(out=b2pad[0:E, :], in_=b2)
+        b2T = const.tile([P, 4, E], F32)
+        pb = pstr.tile([P, 4, P], BF16, tag="tr")
+        for c in range(4):
+            nc.tensor.transpose(pb[:, c, :], b2pad[:, c * P:(c + 1) * P], ident_bf[:])
+        nc.vector.tensor_copy(out=b2T[:], in_=pb[:, :, 0:E])
+
+        hview = h.rearrange("b (g j) s k -> g (j s) b k", j=4)
+        for g in range(4):
+            h_sb = hpool.tile([P, B * H], BF16)
+            nc.sync.dma_start(out=h_sb[:].rearrange("p (b k) -> p b k", b=B), in_=hview[g])
+            hw = h_sb[:].bitcast(F32)
+            hg = hpool.tile([P, B * H], BF16, align_bytes=64)
+            hgw = hg[:].bitcast(F32).rearrange("q (j b s u) -> q b j s u", j=4, b=B, s=S, u=2)
+            for bp in range(2):
+                ph = pstr.tile([P, 2, 2, P], F32, tag="tr")
+                for bb in range(2):
+                    for u in range(2):
+                        col = (2 * bp + bb) * 256 + u * P
+                        nc.tensor.transpose(ph[:, bb, u, :], hw[:, col:col + P], ident_f[:])
+                copy_on(bp == 0, hgw[:, 2 * bp:2 * bp + 2],
+                        ph[:].rearrange("q b u (j s) -> q b j s u", j=4))
+            nc.vector.quantize_mx(out=hq[:, g * 512:(g + 1) * 512].bitcast(FP8X4),
+                                  scales=hs[:, g * 512:(g + 1) * 512], in_=hg[:])
+
+        wview = w2.rearrange("e (u q e2) d -> q (e u) (e2 d)", u=2, e2=2)
+        xview = logits.rearrange("b (c p j) e s -> b c p (j e s)", c=CPB, j=TPC)
+        oview = out.rearrange("b (c p j) d -> b c p (j d)", c=CPB, j=TPC)
+
+        def experts(n):
+            w_raw = wpool.tile([P, 2, 4, D], BF16)
+            nc.sync.dma_start(out=w_raw[:].rearrange("q e (u e2) d -> q (e u) (e2 d)", u=2),
+                              in_=wview[:, 4 * n:4 * n + 4, :])
+            wgs = []
+            for ee in range(2):
+                wg = wgpool.tile([P, D, 4], BF16, align_bytes=64, name="wg%d" % ee)
+                nc.vector.tensor_copy(out=wg[:].rearrange("p (c i) t -> p c t i", i=4),
+                                      in_=w_raw[:, ee].rearrange("p t (c i) -> p c t i", i=4))
+                wgs.append(wg)
+            for ee in range(2):
+                e = 2 * n + ee
+                wq = wgpool.tile([P, D], U32, align_bytes=64, name="wq%d" % ee)
+                ws = wgpool.tile([P, D], U8, align_bytes=64, name="ws%d" % ee)
+                nc.vector.quantize_mx(out=wq[:].bitcast(FP8X4), scales=ws[:],
+                                      in_=wgs[ee][:].rearrange("p d t -> p (d t)"))
+                ps1 = psmm.tile([P, 4, P], F32, tag="mm")
+                for c in range(4):
+                    nc.tensor.matmul_mx(out=ps1[:, c, :],
+                                        lhsT=wq[:, c * P:(c + 1) * P].bitcast(FP8X4),
+                                        lhsT_scale=ws[:, c * P:(c + 1) * P],
+                                        rhs=hq[:, e * P:(e + 1) * P].bitcast(FP8X4),
+                                        rhs_scale=hs[:, e * P:(e + 1) * P],
+                                        start=True, stop=True)
+                for c in range(4):
+                    nc.scalar.activation(out=eoT[:, c, :, e * S:(e + 1) * S],
+                                         in_=ps1[:, c, :].rearrange("p (b s) -> p b s", b=B),
+                                         func=ACT.Identity, bias=b2T[:, c, e:e + 1], scale=1.0)
+
+        live = {}
+
+        def front(i):
+            x = xpool.tile([P, TPC, K], BF16)
+            nc.sync.dma_start(out=x[:].rearrange("p j k -> p (j k)"), in_=xview[i // CPB, i % CPB])
+            t1 = tree.tile([P, TPC, 256], BF16)
+            nc.vector.tensor_tensor(out=t1[:], in0=x[:, :, 0:256], in1=x[:, :, 256:512], op=ALU.max)
+            t2 = tree.tile([P, TPC, 128], BF16)
+            nc.vector.tensor_tensor(out=t2[:], in0=t1[:, :, 0:128], in1=t1[:, :, 128:256], op=ALU.max)
+            t3 = tree.tile([P, TPC, 64], BF16)
+            nc.vector.tensor_tensor(out=t3[:], in0=t2[:, :, 0:64], in1=t2[:, :, 64:128], op=ALU.max)
+            t4 = tree.tile([P, TPC, 32], BF16)
+            nc.vector.tensor_tensor(out=t4[:], in0=t3[:, :, 0:32], in1=t3[:, :, 32:64], op=ALU.max)
+            nm = stat.tile([P, TPC], F32)
+            nc.vector.tensor_reduce(out=nm[:], in_=t4[:], axis=AX.X, op=ALU.max, negate=True)
+            ex = work.tile([P, TPC, K], F32)
+            sm = stat.tile([P, TPC], F32)
+            for j in range(TPC):
+                nc.scalar.activation(out=ex[:, j, :], in_=x[:, j, :], func=ACT.Exp,
+                                     bias=nm[:, j:j + 1], scale=1.0, accum_out=sm[:, j:j + 1])
+            live[i] = (ex, sm)
+
+        def back(i):
+            ex, sm = live[i]
+            rs = stat.tile([P, TPC], F32)
+            nc.vector.reciprocal(out=rs[:], in_=sm[:])
+            cw = work.tile([P, TPC, K], BF16)
+            for j in range(TPC):
+                nc.vector.tensor_scalar(out=cw[:, j, :], in0=ex[:, j, :], scalar1=rs[:, j:j + 1],
+                                        scalar2=None, op0=ALU.mult)
+            live[i] = cw
+
+        def flip(i):
+            cw = live[i]
+            cwg = work.tile([P, TPC, P, 4], BF16, align_bytes=64)
+            for half in range(2):
+                pt = pstr.tile([P, 2, 4, P], BF16, tag="tr")
+                for a in range(2):
+                    for t in range(4):
+                        nc.tensor.transpose(pt[:, a, t, :], cw[:, 2 * half + a, t * P:(t + 1) * P],
+                                            ident_bf[:])
+                copy_on(True, cwg[:, 2 * half:2 * half + 2], pt[:].rearrange("p a t l -> p a l t"))
+            nc.vector.quantize_mx(out=cwq[:, i * 512:(i + 1) * 512].bitcast(FP8X4),
+                                  scales=cws[:, i * 512:(i + 1) * 512],
+                                  in_=cwg[:].rearrange("p a l t -> p (a l t)"))
+
+        def slots(b):
+            eog = work.tile([P, 4, P, 4], BF16, align_bytes=64)
+            for half in range(2):
+                pe = pstr.tile([P, 2, 4, P], BF16, tag="tr")
+                for a in range(2):
+                    for t in range(4):
+                        nc.tensor.transpose(pe[:, a, t, :], eoT[:, 2 * half + a, b, t * P:(t + 1) * P],
+                                            ident_bf[:])
+                copy_on(False, eog[:, 2 * half:2 * half + 2], pe[:].rearrange("p a t d -> p a d t"))
+            nc.vector.quantize_mx(out=eoq[:, b * D:(b + 1) * D].bitcast(FP8X4),
+                                  scales=eos[:, b * D:(b + 1) * D],
+                                  in_=eog[:].rearrange("p a d t -> p (a d t)"))
+
+        def combine(i):
+            b = i // CPB
+            osb = opool.tile([P, TPC, D], F32)
+            for j in range(TPC):
+                po = psmm.tile([P, D], F32, tag="mm")
+                col = i * 512 + j * P
+                nc.tensor.matmul_mx(out=po[:],
+                                    lhsT=cwq[:, col:col + P].bitcast(FP8X4),
+                                    lhsT_scale=cws[:, col:col + P],
+                                    rhs=eoq[:, b * D:(b + 1) * D].bitcast(FP8X4),
+                                    rhs_scale=eos[:, b * D:(b + 1) * D],
+                                    start=True, stop=True)
+                copy_on(j % 2 == 0, osb[:, j, :], po[:])
+            nc.gpsimd.dma_start(out=oview[b, i % CPB], in_=osb[:].rearrange("p j d -> p (j d)"))
+
+        for n in range(8):
+            experts(n)
+            front(n)
+            if n > 0:
+                flip(n - 1)
+            back(n)
+        for b in range(B):
+            slots(b)
+        for m in range(8):
+            front(8 + m)
+            flip(7 + m)
+            back(8 + m)
+            if m < 7:
+                combine(2 * m)
+                combine(2 * m + 1)
+        flip(15)
+        combine(14)
+        combine(15)

@@ -19,35 +19,67 @@ FLOPS = 2 * B * E * S * H * D + 2 * B * L * K * D
 TPC = 4
 NCH = B * L // (P * TPC)
 CPB = NCH // B
+LD_BUFS = 12
+NIT = NCH + 2
 
 
 def tile_softmoe_pb_t_kernel(tc, h, w2, b2, logits, out):
     nc = tc.nc
     with ExitStack() as ctx:
+        ctx.enter_context(tc.manual_schedule())
         const = ctx.enter_context(tc.tile_pool(name="const", bufs=1))
-        hpool = ctx.enter_context(tc.tile_pool(name="hpool", bufs=2))
-        wpool = ctx.enter_context(tc.tile_pool(name="wpool", bufs=3))
-        wgpool = ctx.enter_context(tc.tile_pool(name="wgpool", bufs=2))
-        xpool = ctx.enter_context(tc.tile_pool(name="xpool", bufs=4))
-        tree = ctx.enter_context(tc.tile_pool(name="tree", bufs=2))
-        stat = ctx.enter_context(tc.tile_pool(name="stat", bufs=3))
-        work = ctx.enter_context(tc.tile_pool(name="work", bufs=2))
-        opool = ctx.enter_context(tc.tile_pool(name="opool", bufs=3))
-        pstr = ctx.enter_context(tc.psum_pool(name="pstr", bufs=4))
-        psmm = ctx.enter_context(tc.psum_pool(name="psmm", bufs=4))
+        ld = ctx.enter_context(tc.tile_pool(name="ld", bufs=LD_BUFS))
+        one = ctx.enter_context(tc.tile_pool(name="one", bufs=1))
+        two = ctx.enter_context(tc.tile_pool(name="two", bufs=2))
+        four = ctx.enter_context(tc.tile_pool(name="four", bufs=4))
+        cqp = ctx.enter_context(tc.tile_pool(name="cqp", bufs=10))
+        ps = ctx.enter_context(tc.psum_pool(name="ps", bufs=1))
 
         ident_bf = const.tile([P, P], BF16)
         make_identity(nc, ident_bf[:])
         ident_f = const.tile([P, P], F32)
         make_identity(nc, ident_f[:])
+        b2pad = const.tile([P, D], BF16)
+        nc.gpsimd.memset(b2pad[:], 0.0)
+        nc.scalar.dma_start(out=b2pad[0:E, :], in_=b2)
+        b2T = const.tile([P, 4, E], F32)
 
         hq = const.tile([P, E * P], U32, align_bytes=64)
         hs = const.tile([P, E * P], U8, align_bytes=64)
         eoT = const.tile([P, 4, B, K], BF16)
         eoq = const.tile([P, B * D], U32, align_bytes=64)
         eos = const.tile([P, B * D], U8, align_bytes=64)
-        cwq = const.tile([P, NCH * TPC * P], U32, align_bytes=64)
-        cws = const.tile([P, NCH * TPC * P], U8, align_bytes=64)
+
+        hview = h.rearrange("b (g j) s k -> g (j s) b k", j=4)
+        wview = w2.rearrange("e (u q e2) d -> q (e u) (e2 d)", u=2, e2=2)
+        xview = logits.rearrange("b (c p j) e s -> b c p (j e s)", c=CPB, j=TPC)
+        oview = out.rearrange("b (c p j) d -> b c p (j d)", c=CPB, j=TPC)
+
+        order = [("x", 0), ("w", 0), ("w", 1), ("x", 1), ("h", 0), ("h", 1), ("h", 2), ("h", 3)]
+        for n in range(1, 8):
+            order.extend([("w", 2 * n), ("w", 2 * n + 1), ("x", n + 1)])
+        for i in range(9, NCH):
+            order.append(("x", i))
+        state = {"next": 0, "done": 0}
+        got = {}
+
+        def fill():
+            while state["next"] < len(order) and state["next"] - state["done"] < LD_BUFS:
+                kind, idx = order[state["next"]]
+                t = ld.tile([P, 2048], BF16, name="ldt", tag="ldt")
+                if kind == "x":
+                    nc.sync.dma_start(out=t[:], in_=xview[idx // CPB, idx % CPB])
+                elif kind == "w":
+                    nc.sync.dma_start(out=t[:].rearrange("q (u r) -> q u r", u=2),
+                                      in_=wview[:, 2 * idx:2 * idx + 2, :])
+                else:
+                    nc.sync.dma_start(out=t[:].rearrange("p (b k) -> p b k", b=B), in_=hview[idx])
+                got[(kind, idx)] = t
+                state["next"] = state["next"] + 1
+
+        def free():
+            state["done"] = state["done"] + 1
+            fill()
 
         def copy_on(scalar_engine, dst, src):
             if scalar_engine:
@@ -55,155 +87,242 @@ def tile_softmoe_pb_t_kernel(tc, h, w2, b2, logits, out):
             else:
                 nc.vector.tensor_copy(out=dst, in_=src)
 
-        b2pad = const.tile([P, D], BF16)
-        nc.gpsimd.memset(b2pad[:], 0.0)
-        nc.sync.dma_start(out=b2pad[0:E, :], in_=b2)
-        b2T = const.tile([P, 4, E], F32)
-        pb = pstr.tile([P, 4, P], BF16, tag="tr")
-        for c in range(4):
-            nc.tensor.transpose(pb[:, c, :], b2pad[:, c * P:(c + 1) * P], ident_bf[:])
-        nc.vector.tensor_copy(out=b2T[:], in_=pb[:, :, 0:E])
+        def bank(kind, k, shape, dtype):
+            return ps.tile(shape, dtype, name="%s%d" % (kind, k), tag="%s%d" % (kind, k))
 
-        hview = h.rearrange("b (g j) s k -> g (j s) b k", j=4)
-        for g in range(4):
-            h_sb = hpool.tile([P, B * H], BF16)
-            nc.sync.dma_start(out=h_sb[:].rearrange("p (b k) -> p b k", b=B), in_=hview[g])
-            hw = h_sb[:].bitcast(F32)
-            hg = hpool.tile([P, B * H], BF16, align_bytes=64)
-            hgw = hg[:].bitcast(F32).rearrange("q (j b s u) -> q b j s u", j=4, b=B, s=S, u=2)
+        live = {}
+
+        def t_h(g):
+            hw = got[("h", g)][:].bitcast(F32)
             for bp in range(2):
-                ph = pstr.tile([P, 2, 2, P], F32, tag="tr")
+                ph = bank("tr", (2 * g + bp) % 4, [P, 2, 2, P], F32)
                 for bb in range(2):
                     for u in range(2):
                         col = (2 * bp + bb) * 256 + u * P
                         nc.tensor.transpose(ph[:, bb, u, :], hw[:, col:col + P], ident_f[:])
-                copy_on(bp == 0, hgw[:, 2 * bp:2 * bp + 2],
-                        ph[:].rearrange("q b u (j s) -> q b j s u", j=4))
+                live[("ph", g, bp)] = ph
+            free()
+
+        def he(g):
+            hg = four.tile([P, B * H], BF16, align_bytes=64, name="hg")
+            hgw = hg[:].bitcast(F32).rearrange("q (j b s u) -> q b j s u", j=4, b=B, s=S, u=2)
+            for bp in range(2):
+                copy_on(True, hgw[:, 2 * bp:2 * bp + 2],
+                        live[("ph", g, bp)][:].rearrange("q b u (j s) -> q b j s u", j=4))
+            live[("hg", g)] = hg
+
+        def hquant(g):
             nc.vector.quantize_mx(out=hq[:, g * 512:(g + 1) * 512].bitcast(FP8X4),
-                                  scales=hs[:, g * 512:(g + 1) * 512], in_=hg[:])
+                                  scales=hs[:, g * 512:(g + 1) * 512], in_=live[("hg", g)][:])
 
-        wview = w2.rearrange("e (u q e2) d -> q (e u) (e2 d)", u=2, e2=2)
-        xview = logits.rearrange("b (c p j) e s -> b c p (j e s)", c=CPB, j=TPC)
-        oview = out.rearrange("b (c p j) d -> b c p (j d)", c=CPB, j=TPC)
+        def wr(e):
+            wg = one.tile([P, D, 4], BF16, align_bytes=64, name="wg%d" % (e % 2))
+            nc.vector.tensor_copy(out=wg[:].rearrange("p (c i) t -> p c t i", i=4),
+                                  in_=got[("w", e)][:].rearrange("p (t c i) -> p c t i", t=4, i=4))
+            live[("wg", e)] = wg
+            free()
 
-        def experts(n):
-            w_raw = wpool.tile([P, 2, 4, D], BF16)
-            nc.sync.dma_start(out=w_raw[:].rearrange("q e (u e2) d -> q (e u) (e2 d)", u=2),
-                              in_=wview[:, 4 * n:4 * n + 4, :])
-            wgs = []
-            for ee in range(2):
-                wg = wgpool.tile([P, D, 4], BF16, align_bytes=64, name="wg%d" % ee)
-                nc.vector.tensor_copy(out=wg[:].rearrange("p (c i) t -> p c t i", i=4),
-                                      in_=w_raw[:, ee].rearrange("p t (c i) -> p c t i", i=4))
-                wgs.append(wg)
-            for ee in range(2):
-                e = 2 * n + ee
-                wq = wgpool.tile([P, D], U32, align_bytes=64, name="wq%d" % ee)
-                ws = wgpool.tile([P, D], U8, align_bytes=64, name="ws%d" % ee)
-                nc.vector.quantize_mx(out=wq[:].bitcast(FP8X4), scales=ws[:],
-                                      in_=wgs[ee][:].rearrange("p d t -> p (d t)"))
-                ps1 = psmm.tile([P, 4, P], F32, tag="mm")
-                for c in range(4):
-                    nc.tensor.matmul_mx(out=ps1[:, c, :],
-                                        lhsT=wq[:, c * P:(c + 1) * P].bitcast(FP8X4),
-                                        lhsT_scale=ws[:, c * P:(c + 1) * P],
-                                        rhs=hq[:, e * P:(e + 1) * P].bitcast(FP8X4),
-                                        rhs_scale=hs[:, e * P:(e + 1) * P],
-                                        start=True, stop=True)
-                for c in range(4):
-                    nc.scalar.activation(out=eoT[:, c, :, e * S:(e + 1) * S],
-                                         in_=ps1[:, c, :].rearrange("p (b s) -> p b s", b=B),
-                                         func=ACT.Identity, bias=b2T[:, c, e:e + 1], scale=1.0)
+        def wquant(e):
+            wq = two.tile([P, D], U32, align_bytes=64, name="wq%d" % (e % 2))
+            ws = two.tile([P, D], U8, align_bytes=64, name="ws%d" % (e % 2))
+            nc.vector.quantize_mx(out=wq[:].bitcast(FP8X4), scales=ws[:],
+                                  in_=live[("wg", e)][:].rearrange("p d t -> p (d t)"))
+            live[("wq", e)] = (wq, ws)
 
-        live = {}
+        def mx1(e):
+            wq, ws = live[("wq", e)]
+            ps1 = bank("mm", e % 4, [P, 4, P], F32)
+            for c in range(4):
+                nc.tensor.matmul_mx(out=ps1[:, c, :],
+                                    lhsT=wq[:, c * P:(c + 1) * P].bitcast(FP8X4),
+                                    lhsT_scale=ws[:, c * P:(c + 1) * P],
+                                    rhs=hq[:, e * P:(e + 1) * P].bitcast(FP8X4),
+                                    rhs_scale=hs[:, e * P:(e + 1) * P],
+                                    start=True, stop=True)
+            live[("ps1", e)] = ps1
 
-        def front(i):
-            x = xpool.tile([P, TPC, K], BF16)
-            nc.sync.dma_start(out=x[:].rearrange("p j k -> p (j k)"), in_=xview[i // CPB, i % CPB])
-            t1 = tree.tile([P, TPC, 256], BF16)
+        def e1(e):
+            ps1 = live[("ps1", e)]
+            for c in range(4):
+                nc.scalar.activation(out=eoT[:, c, :, e * S:(e + 1) * S],
+                                     in_=ps1[:, c, :].rearrange("p (b s) -> p b s", b=B),
+                                     func=ACT.Identity, bias=b2T[:, c, e:e + 1], scale=1.0)
+
+        def tr(i):
+            x = got[("x", i)][:].rearrange("p (j k) -> p j k", j=TPC)
+            t1 = one.tile([P, TPC, 256], BF16, name="t1")
             nc.vector.tensor_tensor(out=t1[:], in0=x[:, :, 0:256], in1=x[:, :, 256:512], op=ALU.max)
-            t2 = tree.tile([P, TPC, 128], BF16)
+            t2 = one.tile([P, TPC, 128], BF16, name="t2")
             nc.vector.tensor_tensor(out=t2[:], in0=t1[:, :, 0:128], in1=t1[:, :, 128:256], op=ALU.max)
-            t3 = tree.tile([P, TPC, 64], BF16)
+            t3 = one.tile([P, TPC, 64], BF16, name="t3")
             nc.vector.tensor_tensor(out=t3[:], in0=t2[:, :, 0:64], in1=t2[:, :, 64:128], op=ALU.max)
-            t4 = tree.tile([P, TPC, 32], BF16)
+            t4 = one.tile([P, TPC, 32], BF16, name="t4")
             nc.vector.tensor_tensor(out=t4[:], in0=t3[:, :, 0:32], in1=t3[:, :, 32:64], op=ALU.max)
-            nm = stat.tile([P, TPC], F32)
+            nm = four.tile([P, TPC], F32, name="nm")
             nc.vector.tensor_reduce(out=nm[:], in_=t4[:], axis=AX.X, op=ALU.max, negate=True)
-            ex = work.tile([P, TPC, K], F32)
-            sm = stat.tile([P, TPC], F32)
+            live[("nm", i)] = nm
+
+        def xexp(i):
+            x = got[("x", i)][:].rearrange("p (j k) -> p j k", j=TPC)
+            nm = live[("nm", i)]
+            ex = two.tile([P, TPC, K], F32, name="ex")
+            sm = four.tile([P, TPC], F32, name="sm")
             for j in range(TPC):
                 nc.scalar.activation(out=ex[:, j, :], in_=x[:, j, :], func=ACT.Exp,
                                      bias=nm[:, j:j + 1], scale=1.0, accum_out=sm[:, j:j + 1])
-            live[i] = (ex, sm)
+            live[("ex", i)] = (ex, sm)
+            free()
 
-        def back(i):
-            ex, sm = live[i]
-            rs = stat.tile([P, TPC], F32)
+        def sc(i):
+            ex, sm = live[("ex", i)]
+            rs = two.tile([P, TPC], F32, name="rs")
             nc.vector.reciprocal(out=rs[:], in_=sm[:])
-            cw = work.tile([P, TPC, K], BF16)
+            cw = two.tile([P, TPC, K], BF16, name="cw")
             for j in range(TPC):
                 nc.vector.tensor_scalar(out=cw[:, j, :], in0=ex[:, j, :], scalar1=rs[:, j:j + 1],
                                         scalar2=None, op0=ALU.mult)
-            live[i] = cw
+            live[("cw", i)] = cw
 
-        def flip(i):
-            cw = live[i]
-            cwg = work.tile([P, TPC, P, 4], BF16, align_bytes=64)
+        def t_cw(i):
+            cw = live[("cw", i)]
             for half in range(2):
-                pt = pstr.tile([P, 2, 4, P], BF16, tag="tr")
+                pt = bank("tr", 2 * (i % 2) + half, [P, 2, 4, P], BF16)
                 for a in range(2):
                     for t in range(4):
                         nc.tensor.transpose(pt[:, a, t, :], cw[:, 2 * half + a, t * P:(t + 1) * P],
                                             ident_bf[:])
-                copy_on(True, cwg[:, 2 * half:2 * half + 2], pt[:].rearrange("p a t l -> p a l t"))
-            nc.vector.quantize_mx(out=cwq[:, i * 512:(i + 1) * 512].bitcast(FP8X4),
-                                  scales=cws[:, i * 512:(i + 1) * 512],
-                                  in_=cwg[:].rearrange("p a l t -> p (a l t)"))
+                live[("pt", i, half)] = pt
+            live[("cwg", i)] = two.tile([P, TPC, P, 4], BF16, align_bytes=64, name="cwg")
 
-        def slots(b):
-            eog = work.tile([P, 4, P, 4], BF16, align_bytes=64)
+        def be(i, half, scalar_engine):
+            copy_on(scalar_engine, live[("cwg", i)][:, 2 * half:2 * half + 2],
+                    live[("pt", i, half)][:].rearrange("p a t l -> p a l t"))
+
+        def q(i):
+            cq = cqp.tile([P, 512], U32, align_bytes=64, name="cq")
+            cs = cqp.tile([P, 512], U8, align_bytes=64, name="cs")
+            nc.vector.quantize_mx(out=cq[:].bitcast(FP8X4), scales=cs[:],
+                                  in_=live[("cwg", i)][:].rearrange("p a l t -> p (a l t)"))
+            live[("cq", i)] = (cq, cs)
+
+        def t_eo(b, pair):
             for half in range(2):
-                pe = pstr.tile([P, 2, 4, P], BF16, tag="tr")
+                pe = bank("tr", 2 * pair + half, [P, 2, 4, P], BF16)
                 for a in range(2):
                     for t in range(4):
                         nc.tensor.transpose(pe[:, a, t, :], eoT[:, 2 * half + a, b, t * P:(t + 1) * P],
                                             ident_bf[:])
-                copy_on(False, eog[:, 2 * half:2 * half + 2], pe[:].rearrange("p a t d -> p a d t"))
+                live[("pe", b, half)] = pe
+            live[("eog", b)] = two.tile([P, 4, P, 4], BF16, align_bytes=64, name="eog")
+
+        def eoe(b, half, scalar_engine):
+            copy_on(scalar_engine, live[("eog", b)][:, 2 * half:2 * half + 2],
+                    live[("pe", b, half)][:].rearrange("p a t d -> p a d t"))
+
+        def eoquant(b):
             nc.vector.quantize_mx(out=eoq[:, b * D:(b + 1) * D].bitcast(FP8X4),
                                   scales=eos[:, b * D:(b + 1) * D],
-                                  in_=eog[:].rearrange("p a d t -> p (a d t)"))
+                                  in_=live[("eog", b)][:].rearrange("p a d t -> p (a d t)"))
 
-        def combine(i):
+        def mx2(i):
             b = i // CPB
-            osb = opool.tile([P, TPC, D], F32)
+            cq, cs = live[("cq", i)]
             for j in range(TPC):
-                po = psmm.tile([P, D], F32, tag="mm")
-                col = i * 512 + j * P
+                po = bank("mm", j, [P, D], F32)
                 nc.tensor.matmul_mx(out=po[:],
-                                    lhsT=cwq[:, col:col + P].bitcast(FP8X4),
-                                    lhsT_scale=cws[:, col:col + P],
+                                    lhsT=cq[:, j * P:(j + 1) * P].bitcast(FP8X4),
+                                    lhsT_scale=cs[:, j * P:(j + 1) * P],
                                     rhs=eoq[:, b * D:(b + 1) * D].bitcast(FP8X4),
                                     rhs_scale=eos[:, b * D:(b + 1) * D],
                                     start=True, stop=True)
-                copy_on(j % 2 == 0, osb[:, j, :], po[:])
-            nc.gpsimd.dma_start(out=oview[b, i % CPB], in_=osb[:].rearrange("p j d -> p (j d)"))
+                live[("po", i, j)] = po
+            live[("osb", i)] = four.tile([P, TPC, D], F32, name="osb")
 
-        for n in range(8):
-            experts(n)
-            front(n)
-            if n > 0:
-                flip(n - 1)
-            back(n)
-        for b in range(B):
-            slots(b)
-        for m in range(8):
-            front(8 + m)
-            flip(7 + m)
-            back(8 + m)
-            if m < 7:
-                combine(2 * m)
-                combine(2 * m + 1)
-        flip(15)
-        combine(14)
-        combine(15)
+        def leave(i, on_scalar, pieces):
+            osb = live[("osb", i)]
+            for j in range(TPC):
+                if j not in on_scalar:
+                    copy_on(False, osb[:, j, :], live[("po", i, j)][:])
+            for j in range(TPC):
+                if j in on_scalar:
+                    copy_on(True, osb[:, j, :], live[("po", i, j)][:])
+            flat = osb[:].rearrange("p j d -> p (j d)")
+            w = TPC * D // pieces
+            for s in range(pieces):
+                nc.sync.dma_start(out=oview[i // CPB, i % CPB][:, s * w:(s + 1) * w],
+                                  in_=flat[:, s * w:(s + 1) * w])
+
+        fill()
+        tr(0)
+        for it in range(NIT):
+            prev = it - 1
+            c1 = 2 * (it - 10) + 1 if 10 <= it <= 17 else None
+            c2 = 2 * (it - 9) if 9 <= it <= 16 else None
+            eb = it - 9 if 9 <= it <= 12 else None
+            has_prev = 0 <= prev < NCH
+            if c1 is not None:
+                mx2(c1)
+            if 2 <= it <= 8:
+                mx1(2 * prev)
+                mx1(2 * prev + 1)
+            if eb is not None:
+                t_eo(eb, it % 2)
+            if has_prev:
+                sc(prev)
+                t_cw(prev)
+            if it == 1:
+                for g in range(4):
+                    hquant(g)
+                mx1(0)
+                mx1(1)
+            if it < NCH:
+                xexp(it)
+            if it == 0:
+                pb = bank("tr", 3, [P, 4, P], BF16)
+                for c in range(4):
+                    nc.tensor.transpose(pb[:, c, :], b2pad[:, c * P:(c + 1) * P], ident_bf[:])
+                nc.scalar.copy(out=b2T[:], in_=pb[:, :, 0:E])
+                for g in range(4):
+                    t_h(g)
+                    he(g)
+            if 2 <= it <= 8:
+                e1(2 * prev)
+                e1(2 * prev + 1)
+            if c1 is not None:
+                if it == 16:
+                    leave(c1, (0, 1, 2, 3), 1)
+                elif it == 17:
+                    leave(c1, (1, 3), 2)
+                else:
+                    leave(c1, (3,), 1)
+            if eb is not None:
+                eoe(eb, 0, False)
+                eoe(eb, 1, True)
+            if it < 8:
+                wr(2 * it)
+                wr(2 * it + 1)
+            if it < 8:
+                tr(it + 1)
+            elif it == 8:
+                tr(9)
+                tr(10)
+            elif it + 2 < NCH:
+                tr(it + 2)
+            if it < 8:
+                wquant(2 * it)
+                wquant(2 * it + 1)
+            if has_prev:
+                be(prev, 0, it not in (8, 16))
+                be(prev, 1, True)
+            if it == 1:
+                e1(0)
+                e1(1)
+            if eb is not None:
+                eoquant(eb)
+            if it == 16:
+                q(prev)
+            if c2 is not None:
+                mx2(c2)
+                leave(c2, (3,) if it in (9, 14, 15) else (1, 3), 1)
+            if has_prev and it != 16:
+                q(prev)

@@ -20,7 +20,8 @@ TPC = 4
 NCH = B * L // (P * TPC)
 CPB = NCH // B
 LD_BUFS = 12
-NIT = NCH + 2
+NIT = NCH + 1
+GSC_FROM = 8
 
 
 def tile_softmoe_pb_t_kernel(tc, h, w2, b2, logits, out):
@@ -173,14 +174,22 @@ def tile_softmoe_pb_t_kernel(tc, h, w2, b2, logits, out):
             live[("ex", i)] = (ex, sm)
             free()
 
-        def sc(i):
-            ex, sm = live[("ex", i)]
+        def rc(i):
             rs = two.tile([P, TPC], F32, name="rs")
-            nc.vector.reciprocal(out=rs[:], in_=sm[:])
+            nc.vector.reciprocal(out=rs[:], in_=live[("ex", i)][1][:])
+            live[("rs", i)] = rs
+
+        def sc(i):
+            ex = live[("ex", i)][0]
+            rs = live[("rs", i)]
             cw = two.tile([P, TPC, K], BF16, name="cw")
             for j in range(TPC):
-                nc.vector.tensor_scalar(out=cw[:, j, :], in0=ex[:, j, :], scalar1=rs[:, j:j + 1],
-                                        scalar2=None, op0=ALU.mult)
+                if i >= GSC_FROM:
+                    nc.gpsimd.tensor_scalar(out=cw[:, j, :], in0=ex[:, j, :], scalar1=rs[:, j:j + 1],
+                                            scalar2=0.0, op0=ALU.mult, op1=ALU.add)
+                else:
+                    nc.vector.tensor_scalar(out=cw[:, j, :], in0=ex[:, j, :], scalar1=rs[:, j:j + 1],
+                                            scalar2=None, op0=ALU.mult)
             live[("cw", i)] = cw
 
         def t_cw(i):
@@ -256,25 +265,37 @@ def tile_softmoe_pb_t_kernel(tc, h, w2, b2, logits, out):
         tr(0)
         for it in range(NIT):
             prev = it - 1
-            c1 = 2 * (it - 10) + 1 if 10 <= it <= 17 else None
-            c2 = 2 * (it - 9) if 9 <= it <= 16 else None
+            first = []
+            second = []
+            if it == 9:
+                second = [0, 1]
+            elif 10 <= it <= 15:
+                first = [2 * (it - 9)]
+                second = [2 * (it - 9) + 1]
+            elif it == 16:
+                first = [14]
+                second = [15]
             eb = it - 9 if 9 <= it <= 12 else None
             has_prev = 0 <= prev < NCH
-            if c1 is not None:
-                mx2(c1)
-            if 2 <= it <= 8:
+            share1 = (3,)
+            share2 = (1, 3)
+            if it == 13:
+                share2 = (3,)
+            elif it in (14, 15):
+                share1 = ()
+                share2 = (3,)
+            elif it == 16:
+                share1 = (1, 3)
+            if it == 1:
+                for g in range(4):
+                    hquant(g)
+            for c in first:
+                mx2(c)
+            if 1 <= it <= 8:
                 mx1(2 * prev)
                 mx1(2 * prev + 1)
             if eb is not None:
                 t_eo(eb, it % 2)
-            if has_prev:
-                sc(prev)
-                t_cw(prev)
-            if it == 1:
-                for g in range(4):
-                    hquant(g)
-                mx1(0)
-                mx1(1)
             if it < NCH:
                 xexp(it)
             if it == 0:
@@ -288,13 +309,12 @@ def tile_softmoe_pb_t_kernel(tc, h, w2, b2, logits, out):
             if 2 <= it <= 8:
                 e1(2 * prev)
                 e1(2 * prev + 1)
-            if c1 is not None:
-                if it == 16:
-                    leave(c1, (0, 1, 2, 3), 1)
-                elif it == 17:
-                    leave(c1, (1, 3), 2)
-                else:
-                    leave(c1, (3,), 1)
+            if it == 16:
+                be(prev, 0, False)
+                be(prev, 1, True)
+                q(prev)
+            for c in first:
+                leave(c, share1, 1)
             if eb is not None:
                 eoe(eb, 0, False)
                 eoe(eb, 1, True)
@@ -308,21 +328,27 @@ def tile_softmoe_pb_t_kernel(tc, h, w2, b2, logits, out):
                 tr(10)
             elif it + 2 < NCH:
                 tr(it + 2)
+            if it < NCH and it >= GSC_FROM:
+                rc(it)
+                sc(it)
             if it < 8:
                 wquant(2 * it)
                 wquant(2 * it + 1)
-            if has_prev:
-                be(prev, 0, it not in (8, 16))
+            if has_prev and it != 16:
+                be(prev, 0, it != 8)
                 be(prev, 1, True)
             if it == 1:
                 e1(0)
                 e1(1)
             if eb is not None:
                 eoquant(eb)
-            if it == 16:
-                q(prev)
-            if c2 is not None:
-                mx2(c2)
-                leave(c2, (3,) if it in (9, 14, 15) else (1, 3), 1)
+            for c in second:
+                mx2(c)
+                leave(c, share2, 2 if c == NCH - 1 else 1)
             if has_prev and it != 16:
                 q(prev)
+            if it < NCH and it < GSC_FROM:
+                rc(it)
+                sc(it)
+            if it < NCH:
+                t_cw(it)

@@ -19,9 +19,8 @@ FLOPS = 2 * B * E * S * H * D + 2 * B * L * K * D
 TPC = 4
 NCH = B * L // (P * TPC)
 CPB = NCH // B
-LD_BUFS = 12
-NIT = NCH + 1
-GSC_FROM = 8
+LD_BUFS = 7
+NIT = NCH + 2
 
 
 def tile_softmoe_pb_t_kernel(tc, h, w2, b2, logits, out):
@@ -56,25 +55,26 @@ def tile_softmoe_pb_t_kernel(tc, h, w2, b2, logits, out):
         xview = logits.rearrange("b (c p j) e s -> b c p (j e s)", c=CPB, j=TPC)
         oview = out.rearrange("b (c p j) d -> b c p (j d)", c=CPB, j=TPC)
 
-        order = [("x", 0), ("w", 0), ("w", 1), ("x", 1), ("h", 0), ("h", 1), ("h", 2), ("h", 3)]
-        for n in range(1, 8):
-            order.extend([("w", 2 * n), ("w", 2 * n + 1), ("x", n + 1)])
-        for i in range(9, NCH):
-            order.append(("x", i))
+        order = [("x", 0), ("w", 0), ("h", 0), ("h", 1), ("w", 1), ("x", 1), ("w", 2), ("w", 3), ("x", 2),
+                 ("w", 4), ("w", 5), ("x", 3), ("w", 6), ("w", 7), ("x", 4), ("x", 5), ("x", 6), ("x", 7)]
         state = {"next": 0, "done": 0}
         got = {}
 
         def fill():
             while state["next"] < len(order) and state["next"] - state["done"] < LD_BUFS:
                 kind, idx = order[state["next"]]
-                t = ld.tile([P, 2048], BF16, name="ldt", tag="ldt")
+                t = ld.tile([P, 4096], BF16, name="ldt", tag="ldt")
                 if kind == "x":
-                    nc.sync.dma_start(out=t[:], in_=xview[idx // CPB, idx % CPB])
+                    for a in range(2):
+                        i = 2 * idx + a
+                        nc.sync.dma_start(out=t[:, a * 2048:(a + 1) * 2048], in_=xview[i // CPB, i % CPB])
                 elif kind == "w":
-                    nc.sync.dma_start(out=t[:].rearrange("q (u r) -> q u r", u=2),
-                                      in_=wview[:, 2 * idx:2 * idx + 2, :])
+                    nc.sync.dma_start(out=t[:].rearrange("q (u r) -> q u r", u=4),
+                                      in_=wview[:, 4 * idx:4 * idx + 4, :])
                 else:
-                    nc.sync.dma_start(out=t[:].rearrange("p (b k) -> p b k", b=B), in_=hview[idx])
+                    for a in range(2):
+                        nc.sync.dma_start(out=t[:, a * 2048:(a + 1) * 2048].rearrange("p (b k) -> p b k", b=B),
+                                          in_=hview[2 * idx + a])
                 got[(kind, idx)] = t
                 state["next"] = state["next"] + 1
 
@@ -94,7 +94,7 @@ def tile_softmoe_pb_t_kernel(tc, h, w2, b2, logits, out):
         live = {}
 
         def t_h(g):
-            hw = got[("h", g)][:].bitcast(F32)
+            hw = got[("h", g // 2)][:, (g % 2) * 2048:(g % 2 + 1) * 2048].bitcast(F32)
             for bp in range(2):
                 ph = bank("tr", (2 * g + bp) % 4, [P, 2, 2, P], F32)
                 for bb in range(2):
@@ -102,41 +102,45 @@ def tile_softmoe_pb_t_kernel(tc, h, w2, b2, logits, out):
                         col = (2 * bp + bb) * 256 + u * P
                         nc.tensor.transpose(ph[:, bb, u, :], hw[:, col:col + P], ident_f[:])
                 live[("ph", g, bp)] = ph
-            free()
+            if g % 2 == 1:
+                free()
 
         def he(g):
-            hg = four.tile([P, B * H], BF16, align_bytes=64, name="hg")
-            hgw = hg[:].bitcast(F32).rearrange("q (j b s u) -> q b j s u", j=4, b=B, s=S, u=2)
+            if g % 2 == 0:
+                live[("hg", g // 2)] = two.tile([P, 2 * B * H], BF16, align_bytes=64, name="hg")
+            hg = live[("hg", g // 2)]
+            hgw = hg[:, (g % 2) * 2048:(g % 2 + 1) * 2048].bitcast(F32).rearrange(
+                "q (j b s u) -> q b j s u", j=4, b=B, s=S, u=2)
             for bp in range(2):
                 copy_on(True, hgw[:, 2 * bp:2 * bp + 2],
                         live[("ph", g, bp)][:].rearrange("q b u (j s) -> q b j s u", j=4))
-            live[("hg", g)] = hg
 
-        def hquant(g):
-            nc.vector.quantize_mx(out=hq[:, g * 512:(g + 1) * 512].bitcast(FP8X4),
-                                  scales=hs[:, g * 512:(g + 1) * 512], in_=live[("hg", g)][:])
+        def hquant(g2):
+            nc.vector.quantize_mx(out=hq[:, g2 * 1024:(g2 + 1) * 1024].bitcast(FP8X4),
+                                  scales=hs[:, g2 * 1024:(g2 + 1) * 1024], in_=live[("hg", g2)][:])
 
-        def wr(e):
-            wg = one.tile([P, D, 4], BF16, align_bytes=64, name="wg%d" % (e % 2))
-            nc.vector.tensor_copy(out=wg[:].rearrange("p (c i) t -> p c t i", i=4),
-                                  in_=got[("w", e)][:].rearrange("p (t c i) -> p c t i", t=4, i=4))
-            live[("wg", e)] = wg
+        def wr(n):
+            wg = one.tile([P, 2, D, 4], BF16, align_bytes=64, name="wg")
+            nc.vector.tensor_copy(out=wg[:].rearrange("p e (c i) t -> p e c t i", i=4),
+                                  in_=got[("w", n)][:].rearrange("p (e t c i) -> p e c t i", e=2, t=4, i=4))
+            live[("wg", n)] = wg
             free()
 
-        def wquant(e):
-            wq = two.tile([P, D], U32, align_bytes=64, name="wq%d" % (e % 2))
-            ws = two.tile([P, D], U8, align_bytes=64, name="ws%d" % (e % 2))
+        def wquant(n):
+            wq = two.tile([P, 2 * D], U32, align_bytes=64, name="wq")
+            ws = two.tile([P, 2 * D], U8, align_bytes=64, name="ws")
             nc.vector.quantize_mx(out=wq[:].bitcast(FP8X4), scales=ws[:],
-                                  in_=live[("wg", e)][:].rearrange("p d t -> p (d t)"))
-            live[("wq", e)] = (wq, ws)
+                                  in_=live[("wg", n)][:].rearrange("p e d t -> p (e d t)"))
+            live[("wq", n)] = (wq, ws)
 
         def mx1(e):
-            wq, ws = live[("wq", e)]
+            wq, ws = live[("wq", e // 2)]
             ps1 = bank("mm", e % 4, [P, 4, P], F32)
             for c in range(4):
+                lo = (e % 2) * D + c * P
                 nc.tensor.matmul_mx(out=ps1[:, c, :],
-                                    lhsT=wq[:, c * P:(c + 1) * P].bitcast(FP8X4),
-                                    lhsT_scale=ws[:, c * P:(c + 1) * P],
+                                    lhsT=wq[:, lo:lo + P].bitcast(FP8X4),
+                                    lhsT_scale=ws[:, lo:lo + P],
                                     rhs=hq[:, e * P:(e + 1) * P].bitcast(FP8X4),
                                     rhs_scale=hs[:, e * P:(e + 1) * P],
                                     start=True, stop=True)
@@ -149,22 +153,25 @@ def tile_softmoe_pb_t_kernel(tc, h, w2, b2, logits, out):
                                      in_=ps1[:, c, :].rearrange("p (b s) -> p b s", b=B),
                                      func=ACT.Identity, bias=b2T[:, c, e:e + 1], scale=1.0)
 
-        def tr(i):
-            x = got[("x", i)][:].rearrange("p (j k) -> p j k", j=TPC)
-            t1 = one.tile([P, TPC, 256], BF16, name="t1")
-            nc.vector.tensor_tensor(out=t1[:], in0=x[:, :, 0:256], in1=x[:, :, 256:512], op=ALU.max)
-            t2 = one.tile([P, TPC, 128], BF16, name="t2")
-            nc.vector.tensor_tensor(out=t2[:], in0=t1[:, :, 0:128], in1=t1[:, :, 128:256], op=ALU.max)
-            t3 = one.tile([P, TPC, 64], BF16, name="t3")
-            nc.vector.tensor_tensor(out=t3[:], in0=t2[:, :, 0:64], in1=t2[:, :, 64:128], op=ALU.max)
-            t4 = one.tile([P, TPC, 32], BF16, name="t4")
-            nc.vector.tensor_tensor(out=t4[:], in0=t3[:, :, 0:32], in1=t3[:, :, 32:64], op=ALU.max)
-            nm = four.tile([P, TPC], F32, name="nm")
-            nc.vector.tensor_reduce(out=nm[:], in_=t4[:], axis=AX.X, op=ALU.max, negate=True)
-            live[("nm", i)] = nm
+        def tr(first, count):
+            n = count * TPC
+            lo = (first % 2) * TPC
+            x = got[("x", first // 2)][:].rearrange("p (j k) -> p j k", k=K)[:, lo:lo + n, :]
+            t1 = one.tile([P, 2 * TPC, 256], BF16, name="t1")
+            nc.vector.tensor_tensor(out=t1[:, 0:n], in0=x[:, :, 0:256], in1=x[:, :, 256:512], op=ALU.max)
+            t2 = one.tile([P, 2 * TPC, 128], BF16, name="t2")
+            nc.vector.tensor_tensor(out=t2[:, 0:n], in0=t1[:, 0:n, 0:128], in1=t1[:, 0:n, 128:256], op=ALU.max)
+            t3 = one.tile([P, 2 * TPC, 64], BF16, name="t3")
+            nc.vector.tensor_tensor(out=t3[:, 0:n], in0=t2[:, 0:n, 0:64], in1=t2[:, 0:n, 64:128], op=ALU.max)
+            t4 = one.tile([P, 2 * TPC, 32], BF16, name="t4")
+            nc.vector.tensor_tensor(out=t4[:, 0:n], in0=t3[:, 0:n, 0:32], in1=t3[:, 0:n, 32:64], op=ALU.max)
+            nm = four.tile([P, 2 * TPC], F32, name="nm")
+            nc.vector.tensor_reduce(out=nm[:, 0:n], in_=t4[:, 0:n], axis=AX.X, op=ALU.max, negate=True)
+            for a in range(count):
+                live[("nm", first + a)] = nm[:, a * TPC:(a + 1) * TPC]
 
         def xexp(i):
-            x = got[("x", i)][:].rearrange("p (j k) -> p j k", j=TPC)
+            x = got[("x", i // 2)][:, (i % 2) * 2048:(i % 2 + 1) * 2048].rearrange("p (j k) -> p j k", j=TPC)
             nm = live[("nm", i)]
             ex = two.tile([P, TPC, K], F32, name="ex")
             sm = four.tile([P, TPC], F32, name="sm")
@@ -172,24 +179,17 @@ def tile_softmoe_pb_t_kernel(tc, h, w2, b2, logits, out):
                 nc.scalar.activation(out=ex[:, j, :], in_=x[:, j, :], func=ACT.Exp,
                                      bias=nm[:, j:j + 1], scale=1.0, accum_out=sm[:, j:j + 1])
             live[("ex", i)] = (ex, sm)
-            free()
-
-        def rc(i):
-            rs = two.tile([P, TPC], F32, name="rs")
-            nc.vector.reciprocal(out=rs[:], in_=live[("ex", i)][1][:])
-            live[("rs", i)] = rs
+            if i % 2 == 1:
+                free()
 
         def sc(i):
-            ex = live[("ex", i)][0]
-            rs = live[("rs", i)]
+            ex, sm = live[("ex", i)]
+            rs = two.tile([P, TPC], F32, name="rs")
+            nc.vector.reciprocal(out=rs[:], in_=sm[:])
             cw = two.tile([P, TPC, K], BF16, name="cw")
             for j in range(TPC):
-                if i >= GSC_FROM:
-                    nc.gpsimd.tensor_scalar(out=cw[:, j, :], in0=ex[:, j, :], scalar1=rs[:, j:j + 1],
-                                            scalar2=0.0, op0=ALU.mult, op1=ALU.add)
-                else:
-                    nc.vector.tensor_scalar(out=cw[:, j, :], in0=ex[:, j, :], scalar1=rs[:, j:j + 1],
-                                            scalar2=None, op0=ALU.mult)
+                nc.vector.tensor_scalar(out=cw[:, j, :], in0=ex[:, j, :], scalar1=rs[:, j:j + 1],
+                                        scalar2=None, op0=ALU.mult)
             live[("cw", i)] = cw
 
         def t_cw(i):
@@ -261,41 +261,33 @@ def tile_softmoe_pb_t_kernel(tc, h, w2, b2, logits, out):
                 nc.sync.dma_start(out=oview[i // CPB, i % CPB][:, s * w:(s + 1) * w],
                                   in_=flat[:, s * w:(s + 1) * w])
 
+        PLAN = {10: ((0,), ((1, 3),), (1,), ((3,),)), 11: ((2,), ((1, 2, 3),), (3, 4), ((3,), (1, 3))),
+                12: ((5,), ((3,),), (6,), ((1, 3),)), 13: ((7,), ((3,),), (8,), ((0, 1, 2, 3),)),
+                14: ((9,), ((3,),), (10,), ((3,),)), 15: ((11,), ((3,),), (12,), ((3,),)),
+                16: ((13,), ((0, 1, 2, 3),), (), ()), 17: ((14,), ((1, 2, 3),), (15,), ((1, 3),))}
         fill()
-        tr(0)
+        tr(0, 1)
         for it in range(NIT):
             prev = it - 1
-            first = []
-            second = []
-            if it == 9:
-                second = [0, 1]
-            elif 10 <= it <= 15:
-                first = [2 * (it - 9)]
-                second = [2 * (it - 9) + 1]
-            elif it == 16:
-                first = [14]
-                second = [15]
+            first, share1, second, share2 = PLAN.get(it, ((), (), (), ()))
             eb = it - 9 if 9 <= it <= 12 else None
             has_prev = 0 <= prev < NCH
-            share1 = (3,)
-            share2 = (1, 3)
-            if it == 13:
-                share2 = (3,)
-            elif it in (14, 15):
-                share1 = ()
-                share2 = (3,)
-            elif it == 16:
-                share1 = (1, 3)
-            if it == 1:
-                for g in range(4):
-                    hquant(g)
-            for c in first:
+            last = it >= NCH
+            for c in first[:1]:
                 mx2(c)
-            if 1 <= it <= 8:
+            if 2 <= it <= 8:
                 mx1(2 * prev)
                 mx1(2 * prev + 1)
             if eb is not None:
                 t_eo(eb, it % 2)
+            if has_prev:
+                sc(prev)
+                t_cw(prev)
+            if it == 1:
+                hquant(0)
+                hquant(1)
+                mx1(0)
+                mx1(1)
             if it < NCH:
                 xexp(it)
             if it == 0:
@@ -309,46 +301,33 @@ def tile_softmoe_pb_t_kernel(tc, h, w2, b2, logits, out):
             if 2 <= it <= 8:
                 e1(2 * prev)
                 e1(2 * prev + 1)
-            if it == 16:
-                be(prev, 0, False)
-                be(prev, 1, True)
-                q(prev)
-            for c in first:
-                leave(c, share1, 1)
+            for n, c in enumerate(first):
+                if n > 0:
+                    mx2(c)
+                leave(c, share1[n], 1)
             if eb is not None:
                 eoe(eb, 0, False)
                 eoe(eb, 1, True)
             if it < 8:
-                wr(2 * it)
-                wr(2 * it + 1)
+                wr(it)
+            if it == 0:
+                tr(1, 1)
+            elif it % 2 == 1 and it + 2 < NCH:
+                tr(it + 1, 2)
             if it < 8:
-                tr(it + 1)
-            elif it == 8:
-                tr(9)
-                tr(10)
-            elif it + 2 < NCH:
-                tr(it + 2)
-            if it < NCH and it >= GSC_FROM:
-                rc(it)
-                sc(it)
-            if it < 8:
-                wquant(2 * it)
-                wquant(2 * it + 1)
-            if has_prev and it != 16:
-                be(prev, 0, it != 8)
+                wquant(it)
+            if has_prev:
+                be(prev, 0, it not in (8, 14, 16))
                 be(prev, 1, True)
             if it == 1:
                 e1(0)
                 e1(1)
             if eb is not None:
                 eoquant(eb)
-            for c in second:
-                mx2(c)
-                leave(c, share2, 2 if c == NCH - 1 else 1)
-            if has_prev and it != 16:
+            if last and has_prev:
                 q(prev)
-            if it < NCH and it < GSC_FROM:
-                rc(it)
-                sc(it)
-            if it < NCH:
-                t_cw(it)
+            for n, c in enumerate(second):
+                mx2(c)
+                leave(c, share2[n], 2 if c == NCH - 1 else 1)
+            if has_prev and not last:
+                q(prev)

@@ -26,7 +26,6 @@ NIT = NCH + 2
 def tile_softmoe_pb_t_kernel(tc, h, w2, b2, logits, out):
     nc = tc.nc
     with ExitStack() as ctx:
-        ctx.enter_context(tc.manual_schedule())
         const = ctx.enter_context(tc.tile_pool(name="const", bufs=1))
         ld = ctx.enter_context(tc.tile_pool(name="ld", bufs=LD_BUFS))
         one = ctx.enter_context(tc.tile_pool(name="one", bufs=1))

@@ -32,7 +32,7 @@ def tile_softmoe_pb_t_kernel(tc, h, w2, b2, logits, out):
         two = ctx.enter_context(tc.tile_pool(name="two", bufs=2))
         four = ctx.enter_context(tc.tile_pool(name="four", bufs=4))
         cqp = ctx.enter_context(tc.tile_pool(name="cqp", bufs=10))
-        ps = ctx.enter_context(tc.psum_pool(name="ps", bufs=1))
+        ps = ctx.enter_context(tc.psum_pool(name="ps", bufs=4))
 
         ident_bf = const.tile([P, P], BF16)
         make_identity(nc, ident_bf[:])
@@ -88,7 +88,7 @@ def tile_softmoe_pb_t_kernel(tc, h, w2, b2, logits, out):
                 nc.vector.tensor_copy(out=dst, in_=src)
 
         def bank(kind, k, shape, dtype):
-            return ps.tile(shape, dtype, name="%s%d" % (kind, k), tag="%s%d" % (kind, k))
+            return ps.tile(shape, dtype, name=kind, tag=kind)
 
         live = {}
 
@@ -203,8 +203,8 @@ def tile_softmoe_pb_t_kernel(tc, h, w2, b2, logits, out):
             live[("cwg", i)] = two.tile([P, TPC, P, 4], BF16, align_bytes=64, name="cwg")
 
         def be(i, half, scalar_engine):
-            copy_on(scalar_engine, live[("cwg", i)][:, 2 * half:2 * half + 2],
-                    live[("pt", i, half)][:].rearrange("p a t l -> p a l t"))
+            nc.any.tensor_copy(out=live[("cwg", i)][:, 2 * half:2 * half + 2],
+                               in_=live[("pt", i, half)][:].rearrange("p a t l -> p a l t"))
 
         def q(i):
             cq = cqp.tile([P, 512], U32, align_bytes=64, name="cq")
@@ -224,8 +224,8 @@ def tile_softmoe_pb_t_kernel(tc, h, w2, b2, logits, out):
             live[("eog", b)] = two.tile([P, 4, P, 4], BF16, align_bytes=64, name="eog")
 
         def eoe(b, half, scalar_engine):
-            copy_on(scalar_engine, live[("eog", b)][:, 2 * half:2 * half + 2],
-                    live[("pe", b, half)][:].rearrange("p a t d -> p a d t"))
+            nc.any.tensor_copy(out=live[("eog", b)][:, 2 * half:2 * half + 2],
+                               in_=live[("pe", b, half)][:].rearrange("p a t d -> p a d t"))
 
         def eoquant(b):
             nc.vector.quantize_mx(out=eoq[:, b * D:(b + 1) * D].bitcast(FP8X4),
@@ -249,11 +249,10 @@ def tile_softmoe_pb_t_kernel(tc, h, w2, b2, logits, out):
         def leave(i, on_scalar, pieces):
             osb = live[("osb", i)]
             for j in range(TPC):
-                if j not in on_scalar:
-                    copy_on(False, osb[:, j, :], live[("po", i, j)][:])
-            for j in range(TPC):
-                if j in on_scalar:
-                    copy_on(True, osb[:, j, :], live[("po", i, j)][:])
+                if j % 2 == 1:
+                    nc.scalar.copy(out=osb[:, j, :], in_=live[("po", i, j)][:])
+                else:
+                    nc.any.tensor_copy(out=osb[:, j, :], in_=live[("po", i, j)][:])
             flat = osb[:].rearrange("p j d -> p (j d)")
             w = TPC * D // pieces
             for s in range(pieces):
@@ -327,6 +326,6 @@ def tile_softmoe_pb_t_kernel(tc, h, w2, b2, logits, out):
                 q(prev)
             for n, c in enumerate(second):
                 mx2(c)
-                leave(c, share2[n], 2 if c == NCH - 1 else 1)
+                leave(c, share2[n], 4 if c == NCH - 1 else 1)
             if has_prev and not last:
                 q(prev)

@@ -19,8 +19,10 @@ FLOPS = 2 * B * E * S * H * D + 2 * B * L * K * D
 TPC = 4
 NCH = B * L // (P * TPC)
 CPB = NCH // B
-LD_BUFS = 7
-NIT = NCH + 2
+LD_BUFS = 6
+EX_BUFS = 9
+XA = 12
+AHEAD = 4
 
 
 def tile_softmoe_pb_t_kernel(tc, h, w2, b2, logits, out):
@@ -28,19 +30,25 @@ def tile_softmoe_pb_t_kernel(tc, h, w2, b2, logits, out):
     with ExitStack() as ctx:
         const = ctx.enter_context(tc.tile_pool(name="const", bufs=1))
         ld = ctx.enter_context(tc.tile_pool(name="ld", bufs=LD_BUFS))
+        big = ctx.enter_context(tc.tile_pool(name="big", bufs=EX_BUFS))
         one = ctx.enter_context(tc.tile_pool(name="one", bufs=1))
+        three = ctx.enter_context(tc.tile_pool(name="three", bufs=3))
         two = ctx.enter_context(tc.tile_pool(name="two", bufs=2))
         four = ctx.enter_context(tc.tile_pool(name="four", bufs=4))
-        cqp = ctx.enter_context(tc.tile_pool(name="cqp", bufs=10))
+        stat = ctx.enter_context(tc.tile_pool(name="stat", bufs=8))
+        cqp = ctx.enter_context(tc.tile_pool(name="cqp", bufs=6))
         ps = ctx.enter_context(tc.psum_pool(name="ps", bufs=4))
 
-        ident_bf = const.tile([P, P], BF16)
-        make_identity(nc, ident_bf[:])
-        ident_f = const.tile([P, P], F32)
-        make_identity(nc, ident_f[:])
+        zero = const.tile([P, 1], F32)
+        nc.gpsimd.memset(zero[:], 0.0)
         b2pad = const.tile([P, D], BF16)
         nc.gpsimd.memset(b2pad[:], 0.0)
-        nc.scalar.dma_start(out=b2pad[0:E, :], in_=b2)
+        ident_f = const.tile([P, P], F32)
+        make_identity(nc, ident_f[:])
+        ident_bf = const.tile([P, P], BF16)
+        make_identity(nc, ident_bf[:])
+        warm = const.tile([P, 1], F32)
+        nc.scalar.activation(out=warm[:], in_=zero[:], func=ACT.Exp)
         b2T = const.tile([P, 4, E], F32)
 
         hq = const.tile([P, E * P], U32, align_bytes=64)
@@ -50,82 +58,84 @@ def tile_softmoe_pb_t_kernel(tc, h, w2, b2, logits, out):
         eos = const.tile([P, B * D], U8, align_bytes=64)
 
         hview = h.rearrange("b (g j) s k -> g (j s) b k", j=4)
-        wview = w2.rearrange("e (u q e2) d -> q (e u) (e2 d)", u=2, e2=2)
+        wview = w2.rearrange("e (q t) d -> e q (t d)", t=4)
         xview = logits.rearrange("b (c p j) e s -> b c p (j e s)", c=CPB, j=TPC)
         oview = out.rearrange("b (c p j) d -> b c p (j d)", c=CPB, j=TPC)
 
-        order = [("x", 0), ("w", 0), ("h", 0), ("h", 1), ("w", 1), ("x", 1), ("w", 2), ("w", 3), ("x", 2),
-                 ("w", 4), ("w", 5), ("x", 3), ("w", 6), ("w", 7), ("x", 4), ("x", 5), ("x", 6), ("x", 7)]
+        order = [("x", 0), ("w", 0), ("h", 0), ("w", 1), ("h", 1), ("x", 1), ("w", 2), ("x", 2), ("w", 3), ("x", 3),
+                 ("w", 4), ("x", 4), ("w", 5), ("x", 5), ("w", 6), ("w", 7), ("x", 6), ("x", 7)]
         state = {"next": 0, "done": 0}
         got = {}
+        live = {}
+
+        def load(kind, i):
+            if i % 2 == 0:
+                got[(kind, i // 2)] = ld.tile([P, 4096], BF16, name="ldt", tag="ldt")
+            half = got[(kind, i // 2)][:, (i % 2) * 2048:(i % 2 + 1) * 2048]
+            if kind == "x":
+                nc.sync.dma_start(out=half, in_=xview[i // CPB, i % CPB])
+            elif kind == "w":
+                nc.sync.dma_start(out=half, in_=wview[i])
+            else:
+                nc.sync.dma_start(out=half.rearrange("p (b k) -> p b k", b=B), in_=hview[i])
 
         def fill():
             while state["next"] < len(order) and state["next"] - state["done"] < LD_BUFS:
                 kind, idx = order[state["next"]]
-                t = ld.tile([P, 4096], BF16, name="ldt", tag="ldt")
-                if kind == "x":
-                    for a in range(2):
-                        i = 2 * idx + a
-                        nc.sync.dma_start(out=t[:, a * 2048:(a + 1) * 2048], in_=xview[i // CPB, i % CPB])
-                elif kind == "w":
-                    nc.sync.dma_start(out=t[:].rearrange("q (u r) -> q u r", u=4),
-                                      in_=wview[:, 4 * idx:4 * idx + 4, :])
-                else:
-                    for a in range(2):
-                        nc.sync.dma_start(out=t[:, a * 2048:(a + 1) * 2048].rearrange("p (b k) -> p b k", b=B),
-                                          in_=hview[2 * idx + a])
-                got[(kind, idx)] = t
+                load(kind, 2 * idx)
+                load(kind, 2 * idx + 1)
                 state["next"] = state["next"] + 1
 
         def free():
             state["done"] = state["done"] + 1
             fill()
 
-        def copy_on(scalar_engine, dst, src):
-            if scalar_engine:
-                nc.scalar.copy(out=dst, in_=src)
-            else:
-                nc.vector.tensor_copy(out=dst, in_=src)
-
-        def bank(kind, k, shape, dtype):
+        def bank(kind, shape, dtype):
             return ps.tile(shape, dtype, name=kind, tag=kind)
-
-        live = {}
 
         def t_h(g):
             hw = got[("h", g // 2)][:, (g % 2) * 2048:(g % 2 + 1) * 2048].bitcast(F32)
             for bp in range(2):
-                ph = bank("tr", (2 * g + bp) % 4, [P, 2, 2, P], F32)
+                ph = bank("tr", [P, 2, 2, P], F32)
                 for bb in range(2):
                     for u in range(2):
-                        col = (2 * bp + bb) * 256 + u * P
-                        nc.tensor.transpose(ph[:, bb, u, :], hw[:, col:col + P], ident_f[:])
+                        col = (2 * bp + bb) * 256 + u
+                        nc.tensor.transpose(ph[:, bb, u, :], hw[:, col:col + 255:2], ident_f[:])
                 live[("ph", g, bp)] = ph
             if g % 2 == 1:
                 free()
 
-        def he(g):
-            if g % 2 == 0:
-                live[("hg", g // 2)] = two.tile([P, 2 * B * H], BF16, align_bytes=64, name="hg")
-            hg = live[("hg", g // 2)]
-            hgw = hg[:, (g % 2) * 2048:(g % 2 + 1) * 2048].bitcast(F32).rearrange(
+        def he(g, bp):
+            if g % 2 == 0 and bp == 0:
+                live[("hg", g // 2)] = big.tile([P, 2 * B * H], BF16, align_bytes=64, name="big", tag="big")
+            hgw = live[("hg", g // 2)][:, (g % 2) * 2048:(g % 2 + 1) * 2048].bitcast(F32).rearrange(
                 "q (j b s u) -> q b j s u", j=4, b=B, s=S, u=2)
-            for bp in range(2):
-                copy_on(True, hgw[:, 2 * bp:2 * bp + 2],
-                        live[("ph", g, bp)][:].rearrange("q b u (j s) -> q b j s u", j=4))
+            nc.scalar.copy(out=hgw[:, 2 * bp:2 * bp + 2],
+                           in_=live[("ph", g, bp)][:].rearrange("q b u (j s) -> q b j s u", j=4))
 
-        def hquant(g2):
+        def hq_(g2):
             nc.vector.quantize_mx(out=hq[:, g2 * 1024:(g2 + 1) * 1024].bitcast(FP8X4),
                                   scales=hs[:, g2 * 1024:(g2 + 1) * 1024], in_=live[("hg", g2)][:])
 
-        def wr(n):
-            wg = one.tile([P, 2, D, 4], BF16, align_bytes=64, name="wg")
-            nc.vector.tensor_copy(out=wg[:].rearrange("p e (c i) t -> p e c t i", i=4),
-                                  in_=got[("w", n)][:].rearrange("p (e t c i) -> p e c t i", e=2, t=4, i=4))
-            live[("wg", n)] = wg
-            free()
+        def t_b2():
+            pb = bank("tr", [P, 4, P], BF16)
+            for c in range(4):
+                nc.tensor.transpose(pb[:, c, :], b2pad[:, c * P:(c + 1) * P], ident_bf[:])
+            live["pb"] = pb
 
-        def wquant(n):
+        def b2e():
+            nc.scalar.copy(out=b2T[:], in_=live["pb"][:, :, 0:E])
+
+        def w(n, a):
+            if a == 0:
+                live[("wg", n)] = one.tile([P, 2, D, 4], BF16, align_bytes=64, name="wg")
+            nc.vector.tensor_copy(out=live[("wg", n)][:, a].rearrange("p (c i) t -> p c t i", i=4),
+                                  in_=got[("w", n)][:, a * 2048:(a + 1) * 2048].rearrange(
+                                      "p (t c i) -> p c t i", t=4, i=4))
+            if a == 1:
+                free()
+
+        def wq_(n):
             wq = two.tile([P, 2 * D], U32, align_bytes=64, name="wq")
             ws = two.tile([P, 2 * D], U8, align_bytes=64, name="ws")
             nc.vector.quantize_mx(out=wq[:].bitcast(FP8X4), scales=ws[:],
@@ -134,7 +144,7 @@ def tile_softmoe_pb_t_kernel(tc, h, w2, b2, logits, out):
 
         def mx1(e):
             wq, ws = live[("wq", e // 2)]
-            ps1 = bank("mm", e % 4, [P, 4, P], F32)
+            ps1 = bank("mm", [P, 4, P], F32)
             for c in range(4):
                 lo = (e % 2) * D + c * P
                 nc.tensor.matmul_mx(out=ps1[:, c, :],
@@ -152,180 +162,270 @@ def tile_softmoe_pb_t_kernel(tc, h, w2, b2, logits, out):
                                      in_=ps1[:, c, :].rearrange("p (b s) -> p b s", b=B),
                                      func=ACT.Identity, bias=b2T[:, c, e:e + 1], scale=1.0)
 
-        def tr(first, count):
+        def m(first, count, lev):
             n = count * TPC
             lo = (first % 2) * TPC
-            x = got[("x", first // 2)][:].rearrange("p (j k) -> p j k", k=K)[:, lo:lo + n, :]
-            t1 = one.tile([P, 2 * TPC, 256], BF16, name="t1")
-            nc.vector.tensor_tensor(out=t1[:, 0:n], in0=x[:, :, 0:256], in1=x[:, :, 256:512], op=ALU.max)
-            t2 = one.tile([P, 2 * TPC, 128], BF16, name="t2")
-            nc.vector.tensor_tensor(out=t2[:, 0:n], in0=t1[:, 0:n, 0:128], in1=t1[:, 0:n, 128:256], op=ALU.max)
-            t3 = one.tile([P, 2 * TPC, 64], BF16, name="t3")
-            nc.vector.tensor_tensor(out=t3[:, 0:n], in0=t2[:, 0:n, 0:64], in1=t2[:, 0:n, 64:128], op=ALU.max)
-            t4 = one.tile([P, 2 * TPC, 32], BF16, name="t4")
-            nc.vector.tensor_tensor(out=t4[:, 0:n], in0=t3[:, 0:n, 0:32], in1=t3[:, 0:n, 32:64], op=ALU.max)
-            nm = four.tile([P, 2 * TPC], F32, name="nm")
-            nc.vector.tensor_reduce(out=nm[:, 0:n], in_=t4[:, 0:n], axis=AX.X, op=ALU.max, negate=True)
-            for a in range(count):
-                live[("nm", first + a)] = nm[:, a * TPC:(a + 1) * TPC]
+            if lev == 0:
+                src = got[("x", first // 2)][:].rearrange("p (j k) -> p j k", k=K)[:, lo:lo + n, :]
+            else:
+                src = live[("t", first)]
+            if lev < 4:
+                half = 256 >> lev
+                t = one.tile([P, 2 * TPC, half], BF16, name="t%d" % lev)
+                nc.vector.tensor_tensor(out=t[:, 0:n], in0=src[:, 0:n, 0:half], in1=src[:, 0:n, half:2 * half],
+                                        op=ALU.max)
+                live[("t", first)] = t
+            else:
+                nm = stat.tile([P, 2 * TPC], F32, name="nm")
+                nc.vector.tensor_reduce(out=nm[:, 0:n], in_=src[:, 0:n], axis=AX.X, op=ALU.max, negate=True)
+                for a in range(count):
+                    live[("nm", first + a)] = nm[:, a * TPC:(a + 1) * TPC]
 
-        def xexp(i):
-            x = got[("x", i // 2)][:, (i % 2) * 2048:(i % 2 + 1) * 2048].rearrange("p (j k) -> p j k", j=TPC)
+        def x(i):
+            xt = got[("x", i // 2)][:, (i % 2) * 2048:(i % 2 + 1) * 2048].rearrange("p (j k) -> p j k", j=TPC)
             nm = live[("nm", i)]
-            ex = two.tile([P, TPC, K], F32, name="ex")
-            sm = four.tile([P, TPC], F32, name="sm")
+            ex = big.tile([P, TPC, K], F32, align_bytes=64, name="big", tag="big")
+            sm = stat.tile([P, TPC], F32, name="sm")
             for j in range(TPC):
-                nc.scalar.activation(out=ex[:, j, :], in_=x[:, j, :], func=ACT.Exp,
+                nc.scalar.activation(out=ex[:, j, :], in_=xt[:, j, :], func=ACT.Exp,
                                      bias=nm[:, j:j + 1], scale=1.0, accum_out=sm[:, j:j + 1])
             live[("ex", i)] = (ex, sm)
             if i % 2 == 1:
                 free()
 
-        def sc(i):
+        def sc(i, k):
             ex, sm = live[("ex", i)]
-            rs = two.tile([P, TPC], F32, name="rs")
-            nc.vector.reciprocal(out=rs[:], in_=sm[:])
-            cw = two.tile([P, TPC, K], BF16, name="cw")
-            for j in range(TPC):
-                nc.vector.tensor_scalar(out=cw[:, j, :], in0=ex[:, j, :], scalar1=rs[:, j:j + 1],
-                                        scalar2=None, op0=ALU.mult)
-            live[("cw", i)] = cw
+            if k == 0:
+                rs = two.tile([P, TPC], F32, name="rs")
+                nc.vector.reciprocal(out=rs[:], in_=sm[:])
+                live[("rs", i)] = rs
+                live[("cw", i)] = two.tile([P, TPC, K], BF16, name="cw")
+            else:
+                j = k - 1
+                nc.vector.tensor_scalar(out=live[("cw", i)][:, j, :], in0=ex[:, j, :],
+                                        scalar1=live[("rs", i)][:, j:j + 1], scalar2=None, op0=ALU.mult)
 
-        def t_cw(i):
+        def t(i):
             cw = live[("cw", i)]
             for half in range(2):
-                pt = bank("tr", 2 * (i % 2) + half, [P, 2, 4, P], BF16)
+                pt = bank("tr", [P, 2, 2, P], F32)
                 for a in range(2):
-                    for t in range(4):
-                        nc.tensor.transpose(pt[:, a, t, :], cw[:, 2 * half + a, t * P:(t + 1) * P],
-                                            ident_bf[:])
+                    words = cw[:, 2 * half + a, :].bitcast(F32)
+                    for u in range(2):
+                        nc.tensor.transpose(pt[:, a, u, :], words[:, u:K // 2:2], ident_f[:])
                 live[("pt", i, half)] = pt
-            live[("cwg", i)] = two.tile([P, TPC, P, 4], BF16, align_bytes=64, name="cwg")
 
-        def be(i, half, scalar_engine):
-            nc.any.tensor_copy(out=live[("cwg", i)][:, 2 * half:2 * half + 2],
-                               in_=live[("pt", i, half)][:].rearrange("p a t l -> p a l t"))
+        def be(i, half):
+            if half == 0:
+                live[("cwg", i)] = three.tile([P, TPC, P, 2], F32, align_bytes=64, name="cwg", tag="cwg")
+            nc.scalar.copy(out=live[("cwg", i)][:, 2 * half:2 * half + 2],
+                           in_=live[("pt", i, half)][:].rearrange("p a u l -> p a l u"))
 
         def q(i):
             cq = cqp.tile([P, 512], U32, align_bytes=64, name="cq")
             cs = cqp.tile([P, 512], U8, align_bytes=64, name="cs")
             nc.vector.quantize_mx(out=cq[:].bitcast(FP8X4), scales=cs[:],
-                                  in_=live[("cwg", i)][:].rearrange("p a l t -> p (a l t)"))
+                                  in_=live[("cwg", i)][:].rearrange("p a l u -> p (a l u)").bitcast(BF16))
             live[("cq", i)] = (cq, cs)
 
-        def t_eo(b, pair):
+        def t_eo(b):
             for half in range(2):
-                pe = bank("tr", 2 * pair + half, [P, 2, 4, P], BF16)
+                pe = bank("tr", [P, 2, 2, P], F32)
                 for a in range(2):
-                    for t in range(4):
-                        nc.tensor.transpose(pe[:, a, t, :], eoT[:, 2 * half + a, b, t * P:(t + 1) * P],
-                                            ident_bf[:])
+                    words = eoT[:, 2 * half + a, b, :].bitcast(F32)
+                    for u in range(2):
+                        nc.tensor.transpose(pe[:, a, u, :], words[:, u:K // 2:2], ident_f[:])
                 live[("pe", b, half)] = pe
-            live[("eog", b)] = two.tile([P, 4, P, 4], BF16, align_bytes=64, name="eog")
 
-        def eoe(b, half, scalar_engine):
-            nc.any.tensor_copy(out=live[("eog", b)][:, 2 * half:2 * half + 2],
-                               in_=live[("pe", b, half)][:].rearrange("p a t d -> p a d t"))
+        def eoe(b, half):
+            if half == 0:
+                live[("eog", b)] = three.tile([P, 4, P, 2], F32, align_bytes=64, name="cwg", tag="cwg")
+            nc.scalar.copy(out=live[("eog", b)][:, 2 * half:2 * half + 2],
+                           in_=live[("pe", b, half)][:].rearrange("p a u d -> p a d u"))
 
-        def eoquant(b):
+        def eq(b):
             nc.vector.quantize_mx(out=eoq[:, b * D:(b + 1) * D].bitcast(FP8X4),
                                   scales=eos[:, b * D:(b + 1) * D],
-                                  in_=live[("eog", b)][:].rearrange("p a d t -> p (a d t)"))
+                                  in_=live[("eog", b)][:].rearrange("p a d u -> p (a d u)").bitcast(BF16))
 
-        def mx2(i):
+        def mx2(i, j):
             b = i // CPB
             cq, cs = live[("cq", i)]
-            for j in range(TPC):
-                po = bank("mm", j, [P, D], F32)
-                nc.tensor.matmul_mx(out=po[:],
-                                    lhsT=cq[:, j * P:(j + 1) * P].bitcast(FP8X4),
-                                    lhsT_scale=cs[:, j * P:(j + 1) * P],
-                                    rhs=eoq[:, b * D:(b + 1) * D].bitcast(FP8X4),
-                                    rhs_scale=eos[:, b * D:(b + 1) * D],
-                                    start=True, stop=True)
-                live[("po", i, j)] = po
-            live[("osb", i)] = four.tile([P, TPC, D], F32, name="osb")
+            po = bank("mm", [P, D], F32)
+            nc.tensor.matmul_mx(out=po[:],
+                                lhsT=cq[:, j * P:(j + 1) * P].bitcast(FP8X4),
+                                lhsT_scale=cs[:, j * P:(j + 1) * P],
+                                rhs=eoq[:, b * D:(b + 1) * D].bitcast(FP8X4),
+                                rhs_scale=eos[:, b * D:(b + 1) * D],
+                                start=True, stop=True)
+            live[("po", i, j)] = po
 
-        def leave(i, on_scalar, pieces):
-            osb = live[("osb", i)]
-            for j in range(TPC):
-                if j % 2 == 1:
-                    nc.scalar.copy(out=osb[:, j, :], in_=live[("po", i, j)][:])
-                else:
-                    nc.any.tensor_copy(out=osb[:, j, :], in_=live[("po", i, j)][:])
-            flat = osb[:].rearrange("p j d -> p (j d)")
-            w = TPC * D // pieces
-            for s in range(pieces):
-                nc.sync.dma_start(out=oview[i // CPB, i % CPB][:, s * w:(s + 1) * w],
-                                  in_=flat[:, s * w:(s + 1) * w])
+        left = {}
 
-        PLAN = {10: ((0,), ((1, 3),), (1,), ((3,),)), 11: ((2,), ((1, 2, 3),), (3, 4), ((3,), (1, 3))),
-                12: ((5,), ((3,),), (6,), ((1, 3),)), 13: ((7,), ((3,),), (8,), ((0, 1, 2, 3),)),
-                14: ((9,), ((3,),), (10,), ((3,),)), 15: ((11,), ((3,),), (12,), ((3,),)),
-                16: ((13,), ((0, 1, 2, 3),), (), ()), 17: ((14,), ((1, 2, 3),), (15,), ((1, 3),))}
+        def out_copy(copy, i, j):
+            if ("osb", i, j // 2) not in live:
+                live[("osb", i, j // 2)] = four.tile([P, 2, D], F32, name="osb")
+                left[(i, j // 2)] = 2
+            osb = live[("osb", i, j // 2)]
+            copy(out=osb[:, j % 2, :], in_=live[("po", i, j)][:])
+            left[(i, j // 2)] = left[(i, j // 2)] - 1
+            if left[(i, j // 2)] == 0:
+                nc.sync.dma_start(out=oview[i // CPB, i % CPB][:, 2 * (j // 2) * D:2 * (j // 2 + 1) * D],
+                                  in_=osb[:].rearrange("p j d -> p (j d)"))
+
+        def lv(i, j):
+            out_copy(nc.vector.tensor_copy, i, j)
+
+        def ls(i, j):
+            out_copy(nc.scalar.copy, i, j)
+
+        call = {"t_h": t_h, "he": he, "hq": hq_, "t_b2": t_b2, "b2e": b2e, "w": w, "wq": wq_, "mx1": mx1, "e1": e1,
+                "m": m, "x": x, "sc": sc, "t": t, "be": be, "q": q, "t_eo": t_eo, "eoe": eoe, "eq": eq,
+                "mx2": mx2, "lv": lv, "ls": ls}
+
+        def needs(item):
+            kind = item[0]
+            a = item[1] if len(item) > 1 else 0
+            if kind == "he":
+                return [("t_h", a)]
+            if kind == "hq":
+                return [("he", 2 * a + 1, 1)]
+            if kind == "b2e":
+                return [("t_b2",)]
+            if kind == "wq":
+                return [("w", a, 1)]
+            if kind == "mx1":
+                return [("wq", a // 2), ("hq", a // 8)]
+            if kind == "e1":
+                return [("mx1", a), ("b2e",)]
+            if kind == "x":
+                return [("nm", a)]
+            if kind == "sc":
+                return [("x", a)]
+            if kind == "t":
+                return [("sc", a, 4)]
+            if kind == "be":
+                return [("t", a)]
+            if kind == "q":
+                return [("be", a, 1)]
+            if kind == "t_eo":
+                return [("e1", E - 1)]
+            if kind == "eoe":
+                return [("t_eo", a)]
+            if kind == "eq":
+                return [("eoe", a, 1)]
+            if kind == "mx2":
+                return [("q", a), ("eq", a // CPB)]
+            if kind == "lv" or kind == "ls":
+                return [("mx2", a, item[2])]
+            return []
+
+        def spread(base, extra):
+            merged = []
+            k = 0
+            for n, item in enumerate(base):
+                merged.append(item)
+                while k < len(extra) and (k + 1) * len(base) <= (n + 1) * (len(extra) + 1):
+                    merged.append(extra[k])
+                    k += 1
+            return merged + extra[k:]
+
+        def weave(*parts):
+            merged = []
+            for n in range(max(len(p) for p in parts)):
+                for p in parts:
+                    merged.extend(p[n:n + 1])
+            return merged
+
+        load("x", 0)
+        nc.sync.dma_start(out=b2pad[0:E, :], in_=b2)
+        load("w", 0)
+        load("x", 1)
+        load("w", 1)
+        state["next"] = 2
         fill()
-        tr(0, 1)
-        for it in range(NIT):
-            prev = it - 1
-            first, share1, second, share2 = PLAN.get(it, ((), (), (), ()))
-            eb = it - 9 if 9 <= it <= 12 else None
-            has_prev = 0 <= prev < NCH
-            last = it >= NCH
-            for c in first[:1]:
-                mx2(c)
-            if 2 <= it <= 8:
-                mx1(2 * prev)
-                mx1(2 * prev + 1)
-            if eb is not None:
-                t_eo(eb, it % 2)
-            if has_prev:
-                sc(prev)
-                t_cw(prev)
-            if it == 1:
-                hquant(0)
-                hquant(1)
-                mx1(0)
-                mx1(1)
-            if it < NCH:
-                xexp(it)
-            if it == 0:
-                pb = bank("tr", 3, [P, 4, P], BF16)
-                for c in range(4):
-                    nc.tensor.transpose(pb[:, c, :], b2pad[:, c * P:(c + 1) * P], ident_bf[:])
-                nc.scalar.copy(out=b2T[:], in_=pb[:, :, 0:E])
-                for g in range(4):
-                    t_h(g)
-                    he(g)
-            if 2 <= it <= 8:
-                e1(2 * prev)
-                e1(2 * prev + 1)
-            for n, c in enumerate(first):
-                if n > 0:
-                    mx2(c)
-                leave(c, share1[n], 1)
-            if eb is not None:
-                eoe(eb, 0, False)
-                eoe(eb, 1, True)
-            if it < 8:
-                wr(it)
-            if it == 0:
-                tr(1, 1)
-            elif it % 2 == 1 and it + 2 < NCH:
-                tr(it + 1, 2)
-            if it < 8:
-                wquant(it)
-            if has_prev:
-                be(prev, 0, it not in (8, 14, 16))
-                be(prev, 1, True)
-            if it == 1:
-                e1(0)
-                e1(1)
-            if eb is not None:
-                eoquant(eb)
-            if last and has_prev:
-                q(prev)
-            for n, c in enumerate(second):
-                mx2(c)
-                leave(c, share2[n], 4 if c == NCH - 1 else 1)
-            if has_prev and not last:
-                q(prev)
+        def mm(first, count):
+            return [("m", first, count, lev) for lev in range(5)]
+
+        def ss(i):
+            return [("sc", i, k) for k in range(5)]
+
+        vq = mm(0, 1) + weave([("w", 0, 0), ("w", 0, 1), ("wq", 0)], mm(1, 1))
+        sq = [("x", 0), ("x", 1)] + [("he", g, bp) for g in range(4) for bp in range(2)] + [("b2e",)]
+        pq = [("t_h", g) for g in range(4)] + [("t_b2",), ("mx1", 0), ("mx1", 1)]
+        base = []
+        for n in range(1, 8):
+            base += [("w", n, 0)]
+            base += [("w", n, 1)]
+            base += [("hq", 0)] if n == 1 else []
+            base += [("hq", 1)] if n == 2 else []
+            base += ss(0) if n == 5 else []
+            base += ss(1) if n == 7 else []
+            base += [("wq", n)]
+            pq += [("mx1", 2 * n), ("mx1", 2 * n + 1)]
+            pq += [("t", 0)] if n == 5 else []
+            pq += [("t", 1)] if n == 7 else []
+        vq += spread(base, [it for p in range(1, 6) for it in mm(2 * p, 2)])
+        sb = []
+        for n in range(8):
+            sb += [("e1", 2 * n), ("e1", 2 * n + 1)]
+            sb += [("be", 0, 0), ("be", 0, 1)] if n == 6 else []
+        sq += spread(sb[0:-2], [("x", i) for i in range(2, 12)]) + sb[-2:]
+        pq += [("t_eo", 0)]
+        vq += weave(ss(2), mm(12, 2)) + [("q", 0)]
+        sq += [("eoe", 0, 0), ("eoe", 0, 1), ("be", 1, 0), ("be", 1, 1)]
+        vq += [("eq", 0), ("q", 1)]
+        pq += [("t", 2)]
+        sq += [("x", 12)]
+        X = 13
+        M = 7
+        pq += [("mx2", 0, j) for j in range(4)]
+        LEAD = 3
+        for r in range(NCH):
+            xr = X < NCH and r % 2 == 0
+            vo = [("lv", r, 0), ("lv", r, 2)]
+            so = [("ls", r, 1), ("ls", r, 3)]
+            if False:
+                vo = [("lv", r, 0), ("lv", r, 1), ("lv", r, 2)]
+                so = [("ls", r, 3)]
+            i = r + LEAD
+            vq += vo[0:1]
+            if r % 4 == 2 and r < 12:
+                vq += [("eq", r // 4 + 1)]
+            sc_ = ss(i) if i < NCH else []
+            m_ = []
+            if M < NCH // 2 and X + 2 >= 2 * M:
+                m_ = mm(2 * M, 2)
+                M += 1
+            vq += weave(sc_, m_) if sc_ or m_ else []
+            vq += vo[1:]
+            if i - 1 < NCH:
+                vq += [("q", i - 1)]
+            sq += so[0:1]
+            if i - 1 < NCH:
+                sq += [("be", i - 1, 0), ("be", i - 1, 1)]
+            if r % 4 == 2 and r < 12:
+                sq += [("eoe", r // 4 + 1, 0), ("eoe", r // 4 + 1, 1)]
+            sq += so[1:]
+            if xr:
+                sq += [("x", X)]
+                X += 1
+            if i < NCH:
+                pq += [("t", i)]
+            if r % 4 == 1 and r < 12:
+                pq += [("t_eo", r // 4 + 1)]
+            if r + 1 < NCH:
+                pq += [("mx2", r + 1, j) for j in range(4)]
+        written = set()
+        queues = [vq, sq, pq]
+        while vq or sq or pq:
+            before = len(written)
+            for queue in queues:
+                while queue and all(n in written for n in needs(queue[0])):
+                    item = queue.pop(0)
+                    call[item[0]](*item[1:])
+                    written.add(item)
+                    if item[0] == "m" and item[3] == 4:
+                        for a in range(item[2]):
+                            written.add(("nm", item[1] + a))
+            assert len(written) > before, "no item can be written"

@@ -202,7 +202,8 @@ def tile_softmoe_pb_t_kernel(tc, h, w2, b2, logits, out):
                 live[("cw", i)] = two.tile([P, TPC, K], BF16, name="cw")
             else:
                 j = k - 1
-                nc.vector.tensor_scalar(out=live[("cw", i)][:, j, :], in0=ex[:, j, :],
+                nc.vector.tensor_scalar(out=live[("cw", i)][:, j, :].rearrange("p (u q e) -> p u q e", u=2, e=2),
+                                        in0=ex[:, j, :].rearrange("p (q u e) -> p u q e", u=2, e=2),
                                         scalar1=live[("rs", i)][:, j:j + 1], scalar2=None, op0=ALU.mult)
 
         def t(i):
@@ -212,7 +213,7 @@ def tile_softmoe_pb_t_kernel(tc, h, w2, b2, logits, out):
                 for a in range(2):
                     words = cw[:, 2 * half + a, :].bitcast(F32)
                     for u in range(2):
-                        nc.tensor.transpose(pt[:, a, u, :], words[:, u:K // 2:2], ident_f[:])
+                        nc.tensor.transpose(pt[:, a, u, :], words[:, u * P:(u + 1) * P], ident_f[:])
                 live[("pt", i, half)] = pt
 
         def be(i, half):

@@ -19,9 +19,10 @@ FLOPS = 2 * B * E * S * H * D + 2 * B * L * K * D
 TPC = 4
 NCH = B * L // (P * TPC)
 CPB = NCH // B
-LD_BUFS = 6
-EX_BUFS = 9
+LD_BUFS = 12
+EX_BUFS = 11
 XA = 12
+FINE = 16
 AHEAD = 4
 
 
@@ -34,7 +35,6 @@ def tile_softmoe_pb_t_kernel(tc, h, w2, b2, logits, out):
         one = ctx.enter_context(tc.tile_pool(name="one", bufs=1))
         three = ctx.enter_context(tc.tile_pool(name="three", bufs=3))
         two = ctx.enter_context(tc.tile_pool(name="two", bufs=2))
-        four = ctx.enter_context(tc.tile_pool(name="four", bufs=4))
         stat = ctx.enter_context(tc.tile_pool(name="stat", bufs=8))
         cqp = ctx.enter_context(tc.tile_pool(name="cqp", bufs=6))
         ps = ctx.enter_context(tc.psum_pool(name="ps", bufs=4))
@@ -62,39 +62,42 @@ def tile_softmoe_pb_t_kernel(tc, h, w2, b2, logits, out):
         xview = logits.rearrange("b (c p j) e s -> b c p (j e s)", c=CPB, j=TPC)
         oview = out.rearrange("b (c p j) d -> b c p (j d)", c=CPB, j=TPC)
 
-        order = [("x", 0), ("w", 0), ("h", 0), ("w", 1), ("h", 1), ("x", 1), ("w", 2), ("x", 2), ("w", 3), ("x", 3),
-                 ("w", 4), ("x", 4), ("w", 5), ("x", 5), ("w", 6), ("w", 7), ("x", 6), ("x", 7)]
-        state = {"next": 0, "done": 0}
         got = {}
         live = {}
+        written = set()
+        state = {"issued": 0, "free": LD_BUFS}
 
-        def load(kind, i):
-            if i % 2 == 0:
-                got[(kind, i // 2)] = ld.tile([P, 4096], BF16, name="ldt", tag="ldt")
-            half = got[(kind, i // 2)][:, (i % 2) * 2048:(i % 2 + 1) * 2048]
+        def load(kind, i, parts=1):
+            t = ld.tile([P, 2048], BF16, name="ldt", tag="ldt")
+            got[(kind, i)] = t
             if kind == "x":
-                nc.sync.dma_start(out=half, in_=xview[i // CPB, i % CPB])
+                w = 2048 // parts
+                for a in range(parts):
+                    nc.sync.dma_start(out=t[:, a * w:(a + 1) * w], in_=xview[i // CPB, i % CPB][:, a * w:(a + 1) * w])
             elif kind == "w":
-                nc.sync.dma_start(out=half, in_=wview[i])
+                nc.sync.dma_start(out=t[:], in_=wview[i])
             else:
-                nc.sync.dma_start(out=half.rearrange("p (b k) -> p b k", b=B), in_=hview[i])
+                nc.sync.dma_start(out=t[:].rearrange("p (b k) -> p b k", b=B), in_=hview[i])
+            written.add(("ld", kind, i))
+            state["free"] = state["free"] - 1
+
+        order = [("x", 1), ("w", 0), ("w", 1), ("h", 0), ("h", 1), ("w", 2), ("w", 3), ("x", 2), ("h", 2), ("h", 3), ("x", 3), ("w", 4), ("w", 5), ("x", 4), ("w", 6), ("w", 7), ("x", 5), ("w", 8), ("w", 9), ("x", 6), ("w", 10), ("w", 11), ("x", 7), ("x", 8), ("w", 12), ("w", 13), ("x", 9), ("w", 14), ("w", 15), ("x", 10), ("x", 11), ("x", 12), ("x", 13), ("x", 14), ("x", 15)]
 
         def fill():
-            while state["next"] < len(order) and state["next"] - state["done"] < LD_BUFS:
-                kind, idx = order[state["next"]]
-                load(kind, 2 * idx)
-                load(kind, 2 * idx + 1)
-                state["next"] = state["next"] + 1
+            while state["issued"] < len(order) and state["free"] > 0:
+                kind, i = order[state["issued"]]
+                load(kind, i)
+                state["issued"] = state["issued"] + 1
 
         def free():
-            state["done"] = state["done"] + 1
+            state["free"] = state["free"] + 1
             fill()
 
         def bank(kind, shape, dtype):
             return ps.tile(shape, dtype, name=kind, tag=kind)
 
         def t_h(g):
-            hw = got[("h", g // 2)][:, (g % 2) * 2048:(g % 2 + 1) * 2048].bitcast(F32)
+            hw = got[("h", g)][:].bitcast(F32)
             for bp in range(2):
                 ph = bank("tr", [P, 2, 2, P], F32)
                 for bb in range(2):
@@ -102,8 +105,7 @@ def tile_softmoe_pb_t_kernel(tc, h, w2, b2, logits, out):
                         col = (2 * bp + bb) * 256 + u
                         nc.tensor.transpose(ph[:, bb, u, :], hw[:, col:col + 255:2], ident_f[:])
                 live[("ph", g, bp)] = ph
-            if g % 2 == 1:
-                free()
+            free()
 
         def he(g, bp):
             if g % 2 == 0 and bp == 0:
@@ -127,13 +129,27 @@ def tile_softmoe_pb_t_kernel(tc, h, w2, b2, logits, out):
             nc.scalar.copy(out=b2T[:], in_=live["pb"][:, :, 0:E])
 
         def w(n, a):
-            if a == 0:
+            if ("wg", n) not in live:
                 live[("wg", n)] = one.tile([P, 2, D, 4], BF16, align_bytes=64, name="wg")
             nc.vector.tensor_copy(out=live[("wg", n)][:, a].rearrange("p (c i) t -> p c t i", i=4),
-                                  in_=got[("w", n)][:, a * 2048:(a + 1) * 2048].rearrange(
-                                      "p (t c i) -> p c t i", t=4, i=4))
-            if a == 1:
-                free()
+                                  in_=got[("w", 2 * n + a)][:].rearrange("p (t c i) -> p c t i", t=4, i=4))
+            free()
+
+        def t_w(n, a):
+            src = got[("w", 2 * n + a)][:].rearrange("p (t c) -> p t c", t=4)
+            for half in range(2):
+                pw = bank("tr", [P, 256, 4], BF16)
+                for u in range(4):
+                    nc.tensor.matmul(out=pw[:, :, u], lhsT=ident_bf[:], rhs=src[:, u, half * 256:(half + 1) * 256],
+                                     start=True, stop=True)
+                live[("pw", n, half)] = pw
+            free()
+
+        def we(n, a, half):
+            if ("wg", n) not in live:
+                live[("wg", n)] = one.tile([P, 2, D, 4], BF16, align_bytes=64, name="wg")
+            nc.scalar.copy(out=live[("wg", n)][:, a, half * 256:(half + 1) * 256].rearrange("p c t -> p (c t)").bitcast(F32),
+                           in_=live[("pw", n, half)][:].rearrange("p c t -> p (c t)").bitcast(F32))
 
         def wq_(n):
             wq = two.tile([P, 2 * D], U32, align_bytes=64, name="wq")
@@ -162,35 +178,33 @@ def tile_softmoe_pb_t_kernel(tc, h, w2, b2, logits, out):
                                      in_=ps1[:, c, :].rearrange("p (b s) -> p b s", b=B),
                                      func=ACT.Identity, bias=b2T[:, c, e:e + 1], scale=1.0)
 
-        def m(first, count, lev):
-            n = count * TPC
-            lo = (first % 2) * TPC
-            if lev == 0:
-                src = got[("x", first // 2)][:].rearrange("p (j k) -> p j k", k=K)[:, lo:lo + n, :]
-            else:
-                src = live[("t", first)]
+        def m(i, lev):
+            src = got[("x", i)][:].rearrange("p (j k) -> p j k", k=K) if lev == 0 else live[("t", i)]
             if lev < 4:
                 half = 256 >> lev
-                t = one.tile([P, 2 * TPC, half], BF16, name="t%d" % lev)
-                nc.vector.tensor_tensor(out=t[:, 0:n], in0=src[:, 0:n, 0:half], in1=src[:, 0:n, half:2 * half],
-                                        op=ALU.max)
-                live[("t", first)] = t
+                t = two.tile([P, TPC, half], BF16, name="t%d" % lev)
+                nc.vector.tensor_tensor(out=t[:], in0=src[:, :, 0:half], in1=src[:, :, half:2 * half], op=ALU.max)
+                live[("t", i)] = t
             else:
-                nm = stat.tile([P, 2 * TPC], F32, name="nm")
-                nc.vector.tensor_reduce(out=nm[:, 0:n], in_=src[:, 0:n], axis=AX.X, op=ALU.max, negate=True)
-                for a in range(count):
-                    live[("nm", first + a)] = nm[:, a * TPC:(a + 1) * TPC]
+                nm = stat.tile([P, TPC], F32, name="nm")
+                nc.vector.tensor_reduce(out=nm[:], in_=src[:], axis=AX.X, op=ALU.max, negate=True)
+                live[("nm", i)] = nm
 
-        def x(i):
-            xt = got[("x", i // 2)][:, (i % 2) * 2048:(i % 2 + 1) * 2048].rearrange("p (j k) -> p j k", j=TPC)
-            nm = live[("nm", i)]
-            ex = big.tile([P, TPC, K], F32, align_bytes=64, name="big", tag="big")
-            sm = stat.tile([P, TPC], F32, name="sm")
-            for j in range(TPC):
-                nc.scalar.activation(out=ex[:, j, :], in_=xt[:, j, :], func=ACT.Exp,
-                                     bias=nm[:, j:j + 1], scale=1.0, accum_out=sm[:, j:j + 1])
-            live[("ex", i)] = (ex, sm)
-            if i % 2 == 1:
+        def m0(i, j):
+            if j == 0:
+                live[("nm", i)] = stat.tile([P, TPC], F32, name="nm")
+            nc.vector.tensor_reduce(out=live[("nm", i)][:, j:j + 1], in_=got[("x", i)][:, j * K:(j + 1) * K],
+                                    axis=AX.X, op=ALU.max, negate=True)
+
+        def x(i, j):
+            xt = got[("x", i)][:].rearrange("p (j k) -> p j k", j=TPC)
+            if j == 0:
+                live[("ex", i)] = (big.tile([P, TPC, K], F32, align_bytes=64, name="big", tag="big"),
+                                   stat.tile([P, TPC], F32, name="sm"))
+            ex, sm = live[("ex", i)]
+            nc.scalar.activation(out=ex[:, j, :], in_=xt[:, j, :], func=ACT.Exp,
+                                 bias=live[("nm", i)][:, j:j + 1], scale=1.0, accum_out=sm[:, j:j + 1])
+            if j == TPC - 1:
                 free()
 
         def sc(i, k):
@@ -206,15 +220,14 @@ def tile_softmoe_pb_t_kernel(tc, h, w2, b2, logits, out):
                                         in0=ex[:, j, :].rearrange("p (q u e) -> p u q e", u=2, e=2),
                                         scalar1=live[("rs", i)][:, j:j + 1], scalar2=None, op0=ALU.mult)
 
-        def t(i):
+        def t(i, half):
             cw = live[("cw", i)]
-            for half in range(2):
-                pt = bank("tr", [P, 2, 2, P], F32)
-                for a in range(2):
-                    words = cw[:, 2 * half + a, :].bitcast(F32)
-                    for u in range(2):
-                        nc.tensor.transpose(pt[:, a, u, :], words[:, u * P:(u + 1) * P], ident_f[:])
-                live[("pt", i, half)] = pt
+            pt = bank("tr", [P, 2, 2, P], F32)
+            for a in range(2):
+                words = cw[:, 2 * half + a, :].bitcast(F32)
+                for u in range(2):
+                    nc.tensor.transpose(pt[:, a, u, :], words[:, u * P:(u + 1) * P], ident_f[:])
+            live[("pt", i, half)] = pt
 
         def be(i, half):
             if half == 0:
@@ -222,12 +235,14 @@ def tile_softmoe_pb_t_kernel(tc, h, w2, b2, logits, out):
             nc.scalar.copy(out=live[("cwg", i)][:, 2 * half:2 * half + 2],
                            in_=live[("pt", i, half)][:].rearrange("p a u l -> p a l u"))
 
-        def q(i):
-            cq = cqp.tile([P, 512], U32, align_bytes=64, name="cq")
-            cs = cqp.tile([P, 512], U8, align_bytes=64, name="cs")
-            nc.vector.quantize_mx(out=cq[:].bitcast(FP8X4), scales=cs[:],
-                                  in_=live[("cwg", i)][:].rearrange("p a l u -> p (a l u)").bitcast(BF16))
-            live[("cq", i)] = (cq, cs)
+        def q(i, first, last):
+            if first == 0:
+                live[("cq", i)] = (cqp.tile([P, 512], U32, align_bytes=64, name="cq"),
+                                   cqp.tile([P, 512], U8, align_bytes=64, name="cs"))
+            cq, cs = live[("cq", i)]
+            lo, hi = first * 256, (last + 1) * 256
+            nc.vector.quantize_mx(out=cq[:, lo:hi].bitcast(FP8X4), scales=cs[:, lo:hi],
+                                  in_=live[("cwg", i)][:, 2 * first:2 * last + 2].rearrange("p a l u -> p (a l u)").bitcast(BF16))
 
         def t_eo(b):
             for half in range(2):
@@ -264,15 +279,16 @@ def tile_softmoe_pb_t_kernel(tc, h, w2, b2, logits, out):
         left = {}
 
         def out_copy(copy, i, j):
-            if ("osb", i, j // 2) not in live:
-                live[("osb", i, j // 2)] = four.tile([P, 2, D], F32, name="osb")
-                left[(i, j // 2)] = 2
-            osb = live[("osb", i, j // 2)]
-            copy(out=osb[:, j % 2, :], in_=live[("po", i, j)][:])
-            left[(i, j // 2)] = left[(i, j // 2)] - 1
-            if left[(i, j // 2)] == 0:
-                nc.sync.dma_start(out=oview[i // CPB, i % CPB][:, 2 * (j // 2) * D:2 * (j // 2 + 1) * D],
-                                  in_=osb[:].rearrange("p j d -> p (j d)"))
+            if ("osb", i) not in live:
+                live[("osb", i)] = big.tile([P, TPC, D], F32, align_bytes=64, name="big", tag="big")
+            osb = live[("osb", i)]
+            copy(out=osb[:, j, :], in_=live[("po", i, j)][:])
+            per = 1 if i == NCH - 1 else 2
+            left[(i, j // per)] = left.get((i, j // per), per) - 1
+            if left[(i, j // per)] == 0:
+                lo = j // per * per
+                nc.sync.dma_start(out=oview[i // CPB, i % CPB][:, lo * D:(lo + per) * D],
+                                  in_=osb[:, lo:lo + per].rearrange("p j d -> p (j d)"))
 
         def lv(i, j):
             out_copy(nc.vector.tensor_copy, i, j)
@@ -281,34 +297,46 @@ def tile_softmoe_pb_t_kernel(tc, h, w2, b2, logits, out):
             out_copy(nc.scalar.copy, i, j)
 
         call = {"t_h": t_h, "he": he, "hq": hq_, "t_b2": t_b2, "b2e": b2e, "w": w, "wq": wq_, "mx1": mx1, "e1": e1,
-                "m": m, "x": x, "sc": sc, "t": t, "be": be, "q": q, "t_eo": t_eo, "eoe": eoe, "eq": eq,
+                "m": m, "m0": m0, "t_w": t_w, "we": we, "x": x, "sc": sc, "t": t, "be": be, "q": q, "t_eo": t_eo, "eoe": eoe, "eq": eq,
                 "mx2": mx2, "lv": lv, "ls": ls}
 
         def needs(item):
             kind = item[0]
             a = item[1] if len(item) > 1 else 0
+            if kind == "w":
+                return [("ld", "w", 2 * a + item[2])]
+            if kind == "m":
+                return [("ld", "x", a)] if item[2] == 0 else []
+            if kind == "t_h":
+                return [("ld", "h", a)]
             if kind == "he":
                 return [("t_h", a)]
             if kind == "hq":
                 return [("he", 2 * a + 1, 1)]
             if kind == "b2e":
                 return [("t_b2",)]
+            if kind == "t_w":
+                return [("ld", "w", 2 * a + item[2])]
+            if kind == "we":
+                return [("t_w", a, item[2])]
             if kind == "wq":
-                return [("w", a, 1)]
+                return [("w", a, 0), ("we", a, 1, 1) if a in PEW else ("w", a, 1)]
             if kind == "mx1":
                 return [("wq", a // 2), ("hq", a // 8)]
             if kind == "e1":
                 return [("mx1", a), ("b2e",)]
+            if kind == "m0":
+                return [("ld", "x", a)]
             if kind == "x":
-                return [("nm", a)]
+                return [("m0", a, item[2])] if a in M0 else [("m", a, 4)]
             if kind == "sc":
-                return [("x", a)]
+                return [("x", a, TPC - 1)]
             if kind == "t":
-                return [("sc", a, 4)]
+                return [("sc", a, 2 * item[2] + 2)]
             if kind == "be":
-                return [("t", a)]
+                return [("t", a, item[2])]
             if kind == "q":
-                return [("be", a, 1)]
+                return [("be", a, item[3])]
             if kind == "t_eo":
                 return [("e1", E - 1)]
             if kind == "eoe":
@@ -316,7 +344,7 @@ def tile_softmoe_pb_t_kernel(tc, h, w2, b2, logits, out):
             if kind == "eq":
                 return [("eoe", a, 1)]
             if kind == "mx2":
-                return [("q", a), ("eq", a // CPB)]
+                return [q_items(a)[-1 if item[2] > 1 else 0], ("eq", a // CPB)]
             if kind == "lv" or kind == "ls":
                 return [("mx2", a, item[2])]
             return []
@@ -331,6 +359,9 @@ def tile_softmoe_pb_t_kernel(tc, h, w2, b2, logits, out):
                     k += 1
             return merged + extra[k:]
 
+        def q_items(i):
+            return [("q", i, 0, 0), ("q", i, 1, 1)] if i >= FINE else [("q", i, 0, 1)]
+
         def weave(*parts):
             merged = []
             for n in range(max(len(p) for p in parts)):
@@ -338,86 +369,83 @@ def tile_softmoe_pb_t_kernel(tc, h, w2, b2, logits, out):
                     merged.extend(p[n:n + 1])
             return merged
 
-        load("x", 0)
+        load("x", 0, 2)
         nc.sync.dma_start(out=b2pad[0:E, :], in_=b2)
-        load("w", 0)
-        load("x", 1)
-        load("w", 1)
-        state["next"] = 2
         fill()
-        def mm(first, count):
-            return [("m", first, count, lev) for lev in range(5)]
+        M0 = (0,)
+        PEW = ()
+
+        def mm(i):
+            return [("m", i, lev) for lev in range(5)]
 
         def ss(i):
             return [("sc", i, k) for k in range(5)]
 
-        vq = mm(0, 1) + weave([("w", 0, 0), ("w", 0, 1), ("wq", 0)], mm(1, 1))
-        sq = [("x", 0), ("x", 1)] + [("he", g, bp) for g in range(4) for bp in range(2)] + [("b2e",)]
-        pq = [("t_h", g) for g in range(4)] + [("t_b2",), ("mx1", 0), ("mx1", 1)]
-        base = []
-        for n in range(1, 8):
-            base += [("w", n, 0)]
-            base += [("w", n, 1)]
+        def xx(i):
+            return [("x", i, j) for j in range(TPC)]
+
+        def bb(i):
+            return [("be", i, 0), ("be", i, 1)]
+
+        def tt(i):
+            return [("t", i, 0), ("t", i, 1)]
+
+        vq = [("m0", 0, j) for j in range(TPC)] + mm(1)
+        sq = xx(0) + xx(1)
+        pq = [("t_h", g) for g in range(4)] + [("t_b2",)]
+        he = [("he", g, bp) for g in range(4) for bp in range(2)] + [("b2e",)]
+        for n in range(8):
+            s = n - 6
+            base = q_items(s - 2) if s >= 2 else []
+            base += [("w", n, 0)] if n in PEW else [("w", n, 0), ("w", n, 1)]
             base += [("hq", 0)] if n == 1 else []
             base += [("hq", 1)] if n == 2 else []
-            base += ss(0) if n == 5 else []
-            base += ss(1) if n == 7 else []
+            base += ss(s) if s >= 0 else []
             base += [("wq", n)]
+            vq += spread(base, mm(n + 2))
+            if n == 0:
+                sq += he
+            ee = [("e1", 2 * n - 2), ("e1", 2 * n - 1)] if n > 0 else []
+            if s >= 1:
+                ee += bb(s - 1)
+                pq += tt(s - 1)
+            if n in PEW:
+                pq += [("t_w", n, 1)]
+                sq += [("we", n, 1, 0), ("we", n, 1, 1)]
+            if n > 0:
+                sq += weave(xx(n + 1), ee)
             pq += [("mx1", 2 * n), ("mx1", 2 * n + 1)]
-            pq += [("t", 0)] if n == 5 else []
-            pq += [("t", 1)] if n == 7 else []
-        vq += spread(base, [it for p in range(1, 6) for it in mm(2 * p, 2)])
-        sb = []
-        for n in range(8):
-            sb += [("e1", 2 * n), ("e1", 2 * n + 1)]
-            sb += [("be", 0, 0), ("be", 0, 1)] if n == 6 else []
-        sq += spread(sb[0:-2], [("x", i) for i in range(2, 12)]) + sb[-2:]
-        pq += [("t_eo", 0)]
-        vq += weave(ss(2), mm(12, 2)) + [("q", 0)]
-        sq += [("eoe", 0, 0), ("eoe", 0, 1), ("be", 1, 0), ("be", 1, 1)]
-        vq += [("eq", 0), ("q", 1)]
-        pq += [("t", 2)]
-        sq += [("x", 12)]
-        X = 13
-        M = 7
+        c = 2
+        pq += tt(c - 1) + [("t_eo", 0)]
+        vq += q_items(c - 2) + weave(ss(c), mm(10))
+        sq += bb(c - 1) + [("e1", 14), ("e1", 15)] + xx(9)[0:2] + [("eoe", 0, 0), ("eoe", 0, 1)] + xx(9)[2:4]
+        vq += q_items(c - 1) + [("eq", 0)]
         pq += [("mx2", 0, j) for j in range(4)]
-        LEAD = 3
+        xs = [("x", i, j) for i in range(10, NCH) for j in range(TPC)]
+        ms = [it for i in range(11, NCH) for it in mm(i)]
         for r in range(NCH):
-            xr = X < NCH and r % 2 == 0
-            vo = [("lv", r, 0), ("lv", r, 2)]
-            so = [("ls", r, 1), ("ls", r, 3)]
-            if False:
-                vo = [("lv", r, 0), ("lv", r, 1), ("lv", r, 2)]
-                so = [("ls", r, 3)]
-            i = r + LEAD
-            vq += vo[0:1]
+            i = r + c + 1
+            vv = [("lv", r, 0)] + (q_items(i - 2) if i - 2 < NCH and i - 2 > c - 1 else [])
+            if r % 4 == 3 and r < 12:
+                vv = [("eq", r // 4 + 1)] + vv
+            few = False
+            more = False
+            vv += (ss(i) if i < NCH else []) + ([] if few else [("lv", r, 1), ("lv", r, 2)] if more else [("lv", r, 2)])
+            k = min(len(ms), 3)
+            vq += spread(vv, ms[0:k])
+            ms = ms[k:]
+            bs = bb(i - 1) if i - 1 < NCH else []
             if r % 4 == 2 and r < 12:
-                vq += [("eq", r // 4 + 1)]
-            sc_ = ss(i) if i < NCH else []
-            m_ = []
-            if M < NCH // 2 and X + 2 >= 2 * M:
-                m_ = mm(2 * M, 2)
-                M += 1
-            vq += weave(sc_, m_) if sc_ or m_ else []
-            vq += vo[1:]
+                bs += [("eoe", r // 4 + 1, 0), ("eoe", r // 4 + 1, 1)]
+            k = min(len(xs), 2)
+            sq += weave(([] if more else [("ls", r, 1)]) + xs[0:k], ([("ls", r, 2)] if few else []) + [("ls", r, 3)] + bs)
+            xs = xs[k:]
             if i - 1 < NCH:
-                vq += [("q", i - 1)]
-            sq += so[0:1]
-            if i - 1 < NCH:
-                sq += [("be", i - 1, 0), ("be", i - 1, 1)]
-            if r % 4 == 2 and r < 12:
-                sq += [("eoe", r // 4 + 1, 0), ("eoe", r // 4 + 1, 1)]
-            sq += so[1:]
-            if xr:
-                sq += [("x", X)]
-                X += 1
-            if i < NCH:
-                pq += [("t", i)]
+                pq += tt(i - 1)
             if r % 4 == 1 and r < 12:
                 pq += [("t_eo", r // 4 + 1)]
             if r + 1 < NCH:
                 pq += [("mx2", r + 1, j) for j in range(4)]
-        written = set()
         queues = [vq, sq, pq]
         while vq or sq or pq:
             before = len(written)
@@ -426,7 +454,4 @@ def tile_softmoe_pb_t_kernel(tc, h, w2, b2, logits, out):
                     item = queue.pop(0)
                     call[item[0]](*item[1:])
                     written.add(item)
-                    if item[0] == "m" and item[3] == 4:
-                        for a in range(item[2]):
-                            written.add(("nm", item[1] + a))
-            assert len(written) > before, "no item can be written"
+            assert len(written) > before, str([q[0:2] for q in queues])

@@ -23,6 +23,7 @@ LD_BUFS = 12
 EX_BUFS = 11
 XA = 12
 FINE = 16
+WARM = 480
 AHEAD = 4
 
 
@@ -223,6 +224,8 @@ def tile_softmoe_pb_t_kernel(tc, h, w2, b2, logits, out):
         def t(i, half):
             cw = live[("cw", i)]
             pt = bank("tr", [P, 2, 2, P], F32)
+            nc.tensor.matmul(out=pt[:].rearrange("p a u l -> p (a u l)")[:, 0:WARM], lhsT=ident_bf[:],
+                             rhs=b2pad[:, 0:WARM], start=True, stop=True)
             for a in range(2):
                 words = cw[:, 2 * half + a, :].bitcast(F32)
                 for u in range(2):

@@ -59,7 +59,7 @@ def tile_softmoe_pb_t_kernel(tc, h, w2, b2, logits, out):
         eos = const.tile([P, B * D], U8, align_bytes=64)
 
         hview = h.rearrange("b (g j) s k -> g (j s) b k", j=4)
-        wview = w2.rearrange("e (q t) d -> e q (t d)", t=4)
+        wview = w2.rearrange("e (u q e2) d -> e q u (e2 d)", u=2, e2=2)
         xview = logits.rearrange("b (c p j) e s -> b c p (j e s)", c=CPB, j=TPC)
         oview = out.rearrange("b (c p j) d -> b c p (j d)", c=CPB, j=TPC)
 
@@ -76,13 +76,13 @@ def tile_softmoe_pb_t_kernel(tc, h, w2, b2, logits, out):
                 for a in range(parts):
                     nc.sync.dma_start(out=t[:, a * w:(a + 1) * w], in_=xview[i // CPB, i % CPB][:, a * w:(a + 1) * w])
             elif kind == "w":
-                nc.sync.dma_start(out=t[:], in_=wview[i])
+                nc.sync.dma_start(out=t[:].rearrange("p (u r) -> p u r", u=2), in_=wview[i])
             else:
                 nc.sync.dma_start(out=t[:].rearrange("p (b k) -> p b k", b=B), in_=hview[i])
             written.add(("ld", kind, i))
             state["free"] = state["free"] - 1
 
-        order = [("x", 1), ("w", 0), ("w", 1), ("h", 0), ("h", 1), ("w", 2), ("w", 3), ("x", 2), ("h", 2), ("h", 3), ("x", 3), ("w", 4), ("w", 5), ("x", 4), ("w", 6), ("w", 7), ("x", 5), ("w", 8), ("w", 9), ("x", 6), ("w", 10), ("w", 11), ("x", 7), ("x", 8), ("w", 12), ("w", 13), ("x", 9), ("w", 14), ("w", 15), ("x", 10), ("x", 11), ("x", 12), ("x", 13), ("x", 14), ("x", 15)]
+        order = [("x", 1), ("w", 0), ("w", 1), ("h", 0), ("h", 1), ("x", 2), ("w", 2), ("w", 3), ("h", 2), ("h", 3), ("x", 3), ("w", 4), ("w", 5), ("x", 4), ("w", 6), ("w", 7), ("x", 5), ("w", 8), ("w", 9), ("x", 6), ("w", 10), ("w", 11), ("x", 7), ("x", 8), ("w", 12), ("w", 13), ("x", 9), ("w", 14), ("w", 15), ("x", 10), ("x", 11), ("x", 12), ("x", 13), ("x", 14), ("x", 15)]
 
         def fill():
             while state["issued"] < len(order) and state["free"] > 0:
@@ -103,8 +103,8 @@ def tile_softmoe_pb_t_kernel(tc, h, w2, b2, logits, out):
                 ph = bank("tr", [P, 2, 2, P], F32)
                 for bb in range(2):
                     for u in range(2):
-                        col = (2 * bp + bb) * 256 + u
-                        nc.tensor.transpose(ph[:, bb, u, :], hw[:, col:col + 255:2], ident_f[:])
+                        col = (2 * bp + bb) * 256 + u * P
+                        nc.tensor.transpose(ph[:, bb, u, :], hw[:, col:col + P], ident_f[:])
                 live[("ph", g, bp)] = ph
             free()
 
@@ -217,8 +217,7 @@ def tile_softmoe_pb_t_kernel(tc, h, w2, b2, logits, out):
                 live[("cw", i)] = two.tile([P, TPC, K], BF16, name="cw")
             else:
                 j = k - 1
-                nc.vector.tensor_scalar(out=live[("cw", i)][:, j, :].rearrange("p (u q e) -> p u q e", u=2, e=2),
-                                        in0=ex[:, j, :].rearrange("p (q u e) -> p u q e", u=2, e=2),
+                nc.vector.tensor_scalar(out=live[("cw", i)][:, j, :], in0=ex[:, j, :],
                                         scalar1=live[("rs", i)][:, j:j + 1], scalar2=None, op0=ALU.mult)
 
         def t(i, half):
@@ -253,7 +252,7 @@ def tile_softmoe_pb_t_kernel(tc, h, w2, b2, logits, out):
                 for a in range(2):
                     words = eoT[:, 2 * half + a, b, :].bitcast(F32)
                     for u in range(2):
-                        nc.tensor.transpose(pe[:, a, u, :], words[:, u:K // 2:2], ident_f[:])
+                        nc.tensor.transpose(pe[:, a, u, :], words[:, u * P:(u + 1) * P], ident_f[:])
                 live[("pe", b, half)] = pe
 
         def eoe(b, half):

from contextlib import ExitStack

import concourse.mybir as mybir
from concourse.masks import make_identity

BF16 = mybir.dt.bfloat16
F32 = mybir.dt.float32
U32 = mybir.dt.uint32
U8 = mybir.dt.uint8
FP8X4 = mybir.dt.float8_e4m3fn_x4
ALU = mybir.AluOpType
ACT = mybir.ActivationFunctionType
AX = mybir.AxisListType

P = 128
B, L, D, E, S, H = 4, 2048, 512, 16, 32, 512
K = E * S
FLOPS = 2 * B * E * S * H * D + 2 * B * L * K * D
TPC = 4
NCH = B * L // (P * TPC)
CPB = NCH // B
LD_BUFS = 12
EX_BUFS = 11
XA = 12
FINE = 16
WARM = 480
AHEAD = 4


def tile_softmoe_pb_t_kernel(tc, h, w2, b2, logits, out):
    nc = tc.nc
    with ExitStack() as ctx:
        const = ctx.enter_context(tc.tile_pool(name="const", bufs=1))
        ld = ctx.enter_context(tc.tile_pool(name="ld", bufs=LD_BUFS))
        big = ctx.enter_context(tc.tile_pool(name="big", bufs=EX_BUFS))
        one = ctx.enter_context(tc.tile_pool(name="one", bufs=1))
        three = ctx.enter_context(tc.tile_pool(name="three", bufs=3))
        two = ctx.enter_context(tc.tile_pool(name="two", bufs=2))
        stat = ctx.enter_context(tc.tile_pool(name="stat", bufs=8))
        cqp = ctx.enter_context(tc.tile_pool(name="cqp", bufs=6))
        ps = ctx.enter_context(tc.psum_pool(name="ps", bufs=4))

        zero = const.tile([P, 1], F32)
        nc.gpsimd.memset(zero[:], 0.0)
        b2pad = const.tile([P, D], BF16)
        nc.gpsimd.memset(b2pad[:], 0.0)
        ident_f = const.tile([P, P], F32)
        make_identity(nc, ident_f[:])
        ident_bf = const.tile([P, P], BF16)
        make_identity(nc, ident_bf[:])
        warm = const.tile([P, 1], F32)
        nc.scalar.activation(out=warm[:], in_=zero[:], func=ACT.Exp)
        b2T = const.tile([P, 4, E], F32)

        hq = const.tile([P, E * P], U32, align_bytes=64)
        hs = const.tile([P, E * P], U8, align_bytes=64)
        eoT = const.tile([P, 4, B, K], BF16)
        eoq = const.tile([P, B * D], U32, align_bytes=64)
        eos = const.tile([P, B * D], U8, align_bytes=64)

        hview = h.rearrange("b (g j) s k -> g (j s) b k", j=4)
        wview = w2.rearrange("e (u q e2) d -> e q u (e2 d)", u=2, e2=2)
        xview = logits.rearrange("b (c p j) e s -> b c p (j e s)", c=CPB, j=TPC)
        oview = out.rearrange("b (c p j) d -> b c p (j d)", c=CPB, j=TPC)

        got = {}
        live = {}
        written = set()
        state = {"issued": 0, "free": LD_BUFS}

        def load(kind, i, parts=1):
            t = ld.tile([P, 2048], BF16, name="ldt", tag="ldt")
            got[(kind, i)] = t
            if kind == "x":
                w = 2048 // parts
                for a in range(parts):
                    nc.sync.dma_start(out=t[:, a * w:(a + 1) * w], in_=xview[i // CPB, i % CPB][:, a * w:(a + 1) * w])
            elif kind == "w":
                nc.sync.dma_start(out=t[:].rearrange("p (u r) -> p u r", u=2), in_=wview[i])
            else:
                nc.sync.dma_start(out=t[:].rearrange("p (b k) -> p b k", b=B), in_=hview[i])
            written.add(("ld", kind, i))
            state["free"] = state["free"] - 1

        order = [("x", 1), ("w", 0), ("w", 1), ("h", 0), ("h", 1), ("x", 2), ("w", 2), ("w", 3), ("h", 2), ("h", 3), ("x", 3), ("w", 4), ("w", 5), ("x", 4), ("w", 6), ("w", 7), ("x", 5), ("w", 8), ("w", 9), ("x", 6), ("w", 10), ("w", 11), ("x", 7), ("x", 8), ("w", 12), ("w", 13), ("x", 9), ("w", 14), ("w", 15), ("x", 10), ("x", 11), ("x", 12), ("x", 13), ("x", 14), ("x", 15)]

        def fill():
            while state["issued"] < len(order) and state["free"] > 0:
                kind, i = order[state["issued"]]
                load(kind, i)
                state["issued"] = state["issued"] + 1

        def free():
            state["free"] = state["free"] + 1
            fill()

        def bank(kind, shape, dtype):
            return ps.tile(shape, dtype, name=kind, tag=kind)

        def t_h(g):
            hw = got[("h", g)][:].bitcast(F32)
            for bp in range(2):
                ph = bank("tr", [P, 2, 2, P], F32)
                for bb in range(2):
                    for u in range(2):
                        col = (2 * bp + bb) * 256 + u * P
                        nc.tensor.transpose(ph[:, bb, u, :], hw[:, col:col + P], ident_f[:])
                live[("ph", g, bp)] = ph
            free()

        def he(g, bp):
            if g % 2 == 0 and bp == 0:
                live[("hg", g // 2)] = big.tile([P, 2 * B * H], BF16, align_bytes=64, name="big", tag="big")
            hgw = live[("hg", g // 2)][:, (g % 2) * 2048:(g % 2 + 1) * 2048].bitcast(F32).rearrange(
                "q (j b s u) -> q b j s u", j=4, b=B, s=S, u=2)
            nc.scalar.copy(out=hgw[:, 2 * bp:2 * bp + 2],
                           in_=live[("ph", g, bp)][:].rearrange("q b u (j s) -> q b j s u", j=4))

        def hq_(g2):
            nc.vector.quantize_mx(out=hq[:, g2 * 1024:(g2 + 1) * 1024].bitcast(FP8X4),
                                  scales=hs[:, g2 * 1024:(g2 + 1) * 1024], in_=live[("hg", g2)][:])

        def t_b2():
            pb = bank("tr", [P, 4, P], BF16)
            for c in range(4):
                nc.tensor.transpose(pb[:, c, :], b2pad[:, c * P:(c + 1) * P], ident_bf[:])
            live["pb"] = pb

        def b2e():
            nc.scalar.copy(out=b2T[:], in_=live["pb"][:, :, 0:E])

        def w(n, a):
            if ("wg", n) not in live:
                live[("wg", n)] = one.tile([P, 2, D, 4], BF16, align_bytes=64, name="wg")
            nc.vector.tensor_copy(out=live[("wg", n)][:, a].rearrange("p (c i) t -> p c t i", i=4),
                                  in_=got[("w", 2 * n + a)][:].rearrange("p (t c i) -> p c t i", t=4, i=4))
            free()

        def t_w(n, a):
            src = got[("w", 2 * n + a)][:].rearrange("p (t c) -> p t c", t=4)
            for half in range(2):
                pw = bank("tr", [P, 256, 4], BF16)
                for u in range(4):
                    nc.tensor.matmul(out=pw[:, :, u], lhsT=ident_bf[:], rhs=src[:, u, half * 256:(half + 1) * 256],
                                     start=True, stop=True)
                live[("pw", n, half)] = pw
            free()

        def we(n, a, half):
            if ("wg", n) not in live:
                live[("wg", n)] = one.tile([P, 2, D, 4], BF16, align_bytes=64, name="wg")
            nc.scalar.copy(out=live[("wg", n)][:, a, half * 256:(half + 1) * 256].rearrange("p c t -> p (c t)").bitcast(F32),
                           in_=live[("pw", n, half)][:].rearrange("p c t -> p (c t)").bitcast(F32))

        def wq_(n):
            wq = two.tile([P, 2 * D], U32, align_bytes=64, name="wq")
            ws = two.tile([P, 2 * D], U8, align_bytes=64, name="ws")
            nc.vector.quantize_mx(out=wq[:].bitcast(FP8X4), scales=ws[:],
                                  in_=live[("wg", n)][:].rearrange("p e d t -> p (e d t)"))
            live[("wq", n)] = (wq, ws)

        def mx1(e):
            wq, ws = live[("wq", e // 2)]
            ps1 = bank("mm", [P, 4, P], F32)
            for c in range(4):
                lo = (e % 2) * D + c * P
                nc.tensor.matmul_mx(out=ps1[:, c, :],
                                    lhsT=wq[:, lo:lo + P].bitcast(FP8X4),
                                    lhsT_scale=ws[:, lo:lo + P],
                                    rhs=hq[:, e * P:(e + 1) * P].bitcast(FP8X4),
                                    rhs_scale=hs[:, e * P:(e + 1) * P],
                                    start=True, stop=True)
            live[("ps1", e)] = ps1

        def e1(e):
            ps1 = live[("ps1", e)]
            for c in range(4):
                nc.scalar.activation(out=eoT[:, c, :, e * S:(e + 1) * S],
                                     in_=ps1[:, c, :].rearrange("p (b s) -> p b s", b=B),
                                     func=ACT.Identity, bias=b2T[:, c, e:e + 1], scale=1.0)

        def m(i, lev):
            src = got[("x", i)][:].rearrange("p (j k) -> p j k", k=K) if lev == 0 else live[("t", i)]
            if lev < 4:
                half = 256 >> lev
                t = two.tile([P, TPC, half], BF16, name="t%d" % lev)
                nc.vector.tensor_tensor(out=t[:], in0=src[:, :, 0:half], in1=src[:, :, half:2 * half], op=ALU.max)
                live[("t", i)] = t
            else:
                nm = stat.tile([P, TPC], F32, name="nm")
                nc.vector.tensor_reduce(out=nm[:], in_=src[:], axis=AX.X, op=ALU.max, negate=True)
                live[("nm", i)] = nm

        def m0(i, j):
            if j == 0:
                live[("nm", i)] = stat.tile([P, TPC], F32, name="nm")
            nc.vector.tensor_reduce(out=live[("nm", i)][:, j:j + 1], in_=got[("x", i)][:, j * K:(j + 1) * K],
                                    axis=AX.X, op=ALU.max, negate=True)

        def x(i, j):
            xt = got[("x", i)][:].rearrange("p (j k) -> p j k", j=TPC)
            if j == 0:
                live[("ex", i)] = (big.tile([P, TPC, K], F32, align_bytes=64, name="big", tag="big"),
                                   stat.tile([P, TPC], F32, name="sm"))
            ex, sm = live[("ex", i)]
            nc.scalar.activation(out=ex[:, j, :], in_=xt[:, j, :], func=ACT.Exp,
                                 bias=live[("nm", i)][:, j:j + 1], scale=1.0, accum_out=sm[:, j:j + 1])
            if j == TPC - 1:
                free()

        def sc(i, k):
            ex, sm = live[("ex", i)]
            if k == 0:
                rs = two.tile([P, TPC], F32, name="rs")
                nc.vector.reciprocal(out=rs[:], in_=sm[:])
                live[("rs", i)] = rs
                live[("cw", i)] = two.tile([P, TPC, K], BF16, name="cw")
            else:
                j = k - 1
                nc.vector.tensor_scalar(out=live[("cw", i)][:, j, :], in0=ex[:, j, :],
                                        scalar1=live[("rs", i)][:, j:j + 1], scalar2=None, op0=ALU.mult)

        def t(i, half):
            cw = live[("cw", i)]
            pt = bank("tr", [P, 2, 2, P], F32)
            nc.tensor.matmul(out=pt[:].rearrange("p a u l -> p (a u l)")[:, 0:WARM], lhsT=ident_bf[:],
                             rhs=b2pad[:, 0:WARM], start=True, stop=True)
            for a in range(2):
                words = cw[:, 2 * half + a, :].bitcast(F32)
                for u in range(2):
                    nc.tensor.transpose(pt[:, a, u, :], words[:, u * P:(u + 1) * P], ident_f[:])
            live[("pt", i, half)] = pt

        def be(i, half):
            if half == 0:
                live[("cwg", i)] = three.tile([P, TPC, P, 2], F32, align_bytes=64, name="cwg", tag="cwg")
            nc.scalar.copy(out=live[("cwg", i)][:, 2 * half:2 * half + 2],
                           in_=live[("pt", i, half)][:].rearrange("p a u l -> p a l u"))

        def q(i, first, last):
            if first == 0:
                live[("cq", i)] = (cqp.tile([P, 512], U32, align_bytes=64, name="cq"),
                                   cqp.tile([P, 512], U8, align_bytes=64, name="cs"))
            cq, cs = live[("cq", i)]
            lo, hi = first * 256, (last + 1) * 256
            nc.vector.quantize_mx(out=cq[:, lo:hi].bitcast(FP8X4), scales=cs[:, lo:hi],
                                  in_=live[("cwg", i)][:, 2 * first:2 * last + 2].rearrange("p a l u -> p (a l u)").bitcast(BF16))

        def t_eo(b):
            for half in range(2):
                pe = bank("tr", [P, 2, 2, P], F32)
                for a in range(2):
                    words = eoT[:, 2 * half + a, b, :].bitcast(F32)
                    for u in range(2):
                        nc.tensor.transpose(pe[:, a, u, :], words[:, u * P:(u + 1) * P], ident_f[:])
                live[("pe", b, half)] = pe

        def eoe(b, half):
            if half == 0:
                live[("eog", b)] = three.tile([P, 4, P, 2], F32, align_bytes=64, name="cwg", tag="cwg")
            nc.scalar.copy(out=live[("eog", b)][:, 2 * half:2 * half + 2],
                           in_=live[("pe", b, half)][:].rearrange("p a u d -> p a d u"))

        def eq(b):
            nc.vector.quantize_mx(out=eoq[:, b * D:(b + 1) * D].bitcast(FP8X4),
                                  scales=eos[:, b * D:(b + 1) * D],
                                  in_=live[("eog", b)][:].rearrange("p a d u -> p (a d u)").bitcast(BF16))

        def mx2(i, j):
            b = i // CPB
            cq, cs = live[("cq", i)]
            po = bank("mm", [P, D], F32)
            nc.tensor.matmul_mx(out=po[:],
                                lhsT=cq[:, j * P:(j + 1) * P].bitcast(FP8X4),
                                lhsT_scale=cs[:, j * P:(j + 1) * P],
                                rhs=eoq[:, b * D:(b + 1) * D].bitcast(FP8X4),
                                rhs_scale=eos[:, b * D:(b + 1) * D],
                                start=True, stop=True)
            live[("po", i, j)] = po

        left = {}

        def out_copy(copy, i, j):
            if ("osb", i) not in live:
                live[("osb", i)] = big.tile([P, TPC, D], F32, align_bytes=64, name="big", tag="big")
            osb = live[("osb", i)]
            copy(out=osb[:, j, :], in_=live[("po", i, j)][:])
            per = 1 if i == NCH - 1 else 2
            left[(i, j // per)] = left.get((i, j // per), per) - 1
            if left[(i, j // per)] == 0:
                lo = j // per * per
                nc.sync.dma_start(out=oview[i // CPB, i % CPB][:, lo * D:(lo + per) * D],
                                  in_=osb[:, lo:lo + per].rearrange("p j d -> p (j d)"))

        def lv(i, j):
            out_copy(nc.vector.tensor_copy, i, j)

        def ls(i, j):
            out_copy(nc.scalar.copy, i, j)

        call = {"t_h": t_h, "he": he, "hq": hq_, "t_b2": t_b2, "b2e": b2e, "w": w, "wq": wq_, "mx1": mx1, "e1": e1,
                "m": m, "m0": m0, "t_w": t_w, "we": we, "x": x, "sc": sc, "t": t, "be": be, "q": q, "t_eo": t_eo, "eoe": eoe, "eq": eq,
                "mx2": mx2, "lv": lv, "ls": ls}

        def needs(item):
            kind = item[0]
            a = item[1] if len(item) > 1 else 0
            if kind == "w":
                return [("ld", "w", 2 * a + item[2])]
            if kind == "m":
                return [("ld", "x", a)] if item[2] == 0 else []
            if kind == "t_h":
                return [("ld", "h", a)]
            if kind == "he":
                return [("t_h", a)]
            if kind == "hq":
                return [("he", 2 * a + 1, 1)]
            if kind == "b2e":
                return [("t_b2",)]
            if kind == "t_w":
                return [("ld", "w", 2 * a + item[2])]
            if kind == "we":
                return [("t_w", a, item[2])]
            if kind == "wq":
                return [("w", a, 0), ("we", a, 1, 1) if a in PEW else ("w", a, 1)]
            if kind == "mx1":
                return [("wq", a // 2), ("hq", a // 8)]
            if kind == "e1":
                return [("mx1", a), ("b2e",)]
            if kind == "m0":
                return [("ld", "x", a)]
            if kind == "x":
                return [("m0", a, item[2])] if a in M0 else [("m", a, 4)]
            if kind == "sc":
                return [("x", a, TPC - 1)]
            if kind == "t":
                return [("sc", a, 2 * item[2] + 2)]
            if kind == "be":
                return [("t", a, item[2])]
            if kind == "q":
                return [("be", a, item[3])]
            if kind == "t_eo":
                return [("e1", E - 1)]
            if kind == "eoe":
                return [("t_eo", a)]
            if kind == "eq":
                return [("eoe", a, 1)]
            if kind == "mx2":
                return [q_items(a)[-1 if item[2] > 1 else 0], ("eq", a // CPB)]
            if kind == "lv" or kind == "ls":
                return [("mx2", a, item[2])]
            return []

        def spread(base, extra):
            merged = []
            k = 0
            for n, item in enumerate(base):
                merged.append(item)
                while k < len(extra) and (k + 1) * len(base) <= (n + 1) * (len(extra) + 1):
                    merged.append(extra[k])
                    k += 1
            return merged + extra[k:]

        def q_items(i):
            return [("q", i, 0, 0), ("q", i, 1, 1)] if i >= FINE else [("q", i, 0, 1)]

        def weave(*parts):
            merged = []
            for n in range(max(len(p) for p in parts)):
                for p in parts:
                    merged.extend(p[n:n + 1])
            return merged

        load("x", 0, 2)
        nc.sync.dma_start(out=b2pad[0:E, :], in_=b2)
        fill()
        M0 = (0,)
        PEW = ()

        def mm(i):
            return [("m", i, lev) for lev in range(5)]

        def ss(i):
            return [("sc", i, k) for k in range(5)]

        def xx(i):
            return [("x", i, j) for j in range(TPC)]

        def bb(i):
            return [("be", i, 0), ("be", i, 1)]

        def tt(i):
            return [("t", i, 0), ("t", i, 1)]

        vq = [("m0", 0, j) for j in range(TPC)] + mm(1)
        sq = xx(0) + xx(1)
        pq = [("t_h", g) for g in range(4)] + [("t_b2",)]
        he = [("he", g, bp) for g in range(4) for bp in range(2)] + [("b2e",)]
        for n in range(8):
            s = n - 6
            base = q_items(s - 2) if s >= 2 else []
            base += [("w", n, 0)] if n in PEW else [("w", n, 0), ("w", n, 1)]
            base += [("hq", 0)] if n == 1 else []
            base += [("hq", 1)] if n == 2 else []
            base += ss(s) if s >= 0 else []
            base += [("wq", n)]
            vq += spread(base, mm(n + 2))
            if n == 0:
                sq += he
            ee = [("e1", 2 * n - 2), ("e1", 2 * n - 1)] if n > 0 else []
            if s >= 1:
                ee += bb(s - 1)
                pq += tt(s - 1)
            if n in PEW:
                pq += [("t_w", n, 1)]
                sq += [("we", n, 1, 0), ("we", n, 1, 1)]
            if n > 0:
                sq += weave(xx(n + 1), ee)
            pq += [("mx1", 2 * n), ("mx1", 2 * n + 1)]
        c = 2
        pq += tt(c - 1) + [("t_eo", 0)]
        vq += q_items(c - 2) + weave(ss(c), mm(10))
        sq += bb(c - 1) + [("e1", 14), ("e1", 15)] + xx(9)[0:2] + [("eoe", 0, 0), ("eoe", 0, 1)] + xx(9)[2:4]
        vq += q_items(c - 1) + [("eq", 0)]
        pq += [("mx2", 0, j) for j in range(4)]
        xs = [("x", i, j) for i in range(10, NCH) for j in range(TPC)]
        ms = [it for i in range(11, NCH) for it in mm(i)]
        for r in range(NCH):
            i = r + c + 1
            vv = [("lv", r, 0)] + (q_items(i - 2) if i - 2 < NCH and i - 2 > c - 1 else [])
            if r % 4 == 3 and r < 12:
                vv = [("eq", r // 4 + 1)] + vv
            few = False
            more = False
            vv += (ss(i) if i < NCH else []) + ([] if few else [("lv", r, 1), ("lv", r, 2)] if more else [("lv", r, 2)])
            k = min(len(ms), 3)
            vq += spread(vv, ms[0:k])
            ms = ms[k:]
            bs = bb(i - 1) if i - 1 < NCH else []
            if r % 4 == 2 and r < 12:
                bs += [("eoe", r // 4 + 1, 0), ("eoe", r // 4 + 1, 1)]
            k = min(len(xs), 2)
            sq += weave(([] if more else [("ls", r, 1)]) + xs[0:k], ([("ls", r, 2)] if few else []) + [("ls", r, 3)] + bs)
            xs = xs[k:]
            if i - 1 < NCH:
                pq += tt(i - 1)
            if r % 4 == 1 and r < 12:
                pq += [("t_eo", r // 4 + 1)]
            if r + 1 < NCH:
                pq += [("mx2", r + 1, j) for j in range(4)]
        queues = [vq, sq, pq]
        while vq or sq or pq:
            before = len(written)
            for queue in queues:
                while queue and all(n in written for n in needs(queue[0])):
                    item = queue.pop(0)
                    call[item[0]](*item[1:])
                    written.add(item)
            assert len(written) > before, str([q[0:2] for q in queues])
